import numpy as np
import ml_dtypes


def mxq(x, axis, fmt="e4m3"):
    dtype, down = {"e4m3": (ml_dtypes.float8_e4m3fn, 7), "e5m2": (ml_dtypes.float8_e5m2, 14)}[fmt]
    v = np.moveaxis(np.asarray(x, np.float32).astype(ml_dtypes.bfloat16).astype(np.float64), axis, -1)
    blocks = v.reshape(v.shape[:-1] + (-1, 32))
    amax = np.abs(blocks).max(-1, keepdims=True)
    byte = np.maximum(np.where(amax > 0, np.frexp(amax)[1] - 1 + 127, 0) - down, 1)
    scale = np.exp2(byte - 127.0)
    codes = (blocks / scale).astype(np.float32).astype(dtype).astype(np.float64)
    return np.moveaxis((codes * scale).reshape(v.shape), -1, axis)


WIDE = False


def mx_kscale(k):
    if not WIDE:
        return np.ones(k)
    levels = np.array([10, -10, 5, -5, 0])
    a = np.random.permutation(np.resize(levels, k // 512 * 4)).reshape(k // 512, 4)
    idx = np.arange(k)
    return np.exp2(a[idx // 512, idx % 128 // 32])


BF16 = ml_dtypes.bfloat16


def bf(x):
    return np.asarray(x, np.float32).astype(BF16)


def f64(x):
    return np.asarray(x).astype(np.float64)


N, D, T, O = 4096, 512, 1024, 128
LEAKY_SLOPE = 0.01
P_EDGE = 0.25
ZS = np.sqrt(N) / 8.0


def setup_inputs():
    s = mx_kscale(D)
    edges = np.random.random((N, N)) < P_EDGE
    return {"A1": bf((0.1 + 0.9 * np.random.random((N, N))) * edges + np.eye(N)),
            "Hn": bf(np.random.standard_normal((N, D)) * s),
            "Wout": bf(np.random.standard_normal((D, O)) * ZS / np.sqrt(D) / s[:, None]),
            "bout": bf(0.1 * np.random.standard_normal(O) - 0.2)}


def reference(A1, Hn, Wout, bout):
    A = f64(A1)
    d = np.power(A.sum(axis=1), -0.5)
    A_hat = A * d[:, None] * d[None, :]
    Z = (mxq(f64(Hn), 1, "e4m3") @ mxq(f64(Wout), 0, "e4m3")) + f64(bout)
    y = mxq(A_hat, 1, "e4m3") @ mxq(Z, 0, "e4m3")
    return np.where(y >= 0, y, LEAKY_SLOPE * y)

@@ -1,0 +1,281 @@
+from contextlib import ExitStack
+
+import concourse.mybir as mybir
+from concourse.masks import make_identity
+
+F32 = mybir.dt.float32
+BF16 = mybir.dt.bfloat16
+U32 = mybir.dt.uint32
+U8 = mybir.dt.uint8
+FP8X4 = mybir.dt.float8_e4m3fn_x4
+ALU = mybir.AluOpType
+ACT = mybir.ActivationFunctionType
+
+P = 128
+PACK = 4
+K_PASS = P * PACK
+N_NODES = 4096
+N_FEAT = 512
+N_OUT = 128
+LEAKY_SLOPE = 0.01
+
+ROW_TILES = N_NODES // P
+HALF = N_NODES // 2
+PASSES_PER_UNIT = HALF // K_PASS
+UNITS = 2 * ROW_TILES
+GROUP_TILES = 8
+GROUPS = ROW_TILES // GROUP_TILES
+VECTOR_SUM_COLS = 1344
+LAG = 2
+TILES_PER_BANK = 4
+
+FLOPS = 2 * N_NODES * N_FEAT * N_OUT + 2 * N_NODES * N_NODES * N_OUT
+
+
+def tile_gcnlayer_pb_t_kernel(tc, A1, Hn, Wout, bout, out):
+    nc = tc.nc
+    with ExitStack() as ctx:
+        keep = ctx.enter_context(tc.tile_pool(name="keep", bufs=1))
+        xpool = ctx.enter_context(tc.tile_pool(name="xpool", bufs=6))
+        psum_t = ctx.enter_context(tc.psum_pool(name="psum_t", bufs=5))
+        psum_acc = ctx.enter_context(tc.psum_pool(name="psum_acc", bufs=3))
+
+        ident_bf = keep.tile([P, P], BF16)
+        make_identity(nc, ident_bf[:])
+        ident_f = keep.tile([P, P], F32)
+        make_identity(nc, ident_f[:])
+
+        one = keep.tile([P, 1], F32)
+        nc.vector.memset(one[:], 1.0)
+        warm = keep.tile([P, 1], F32)
+        nc.scalar.sqrt(warm[:], one[:])
+
+        z_codes = keep.tile([P, N_NODES // K_PASS, N_OUT], U32, align_bytes=64)
+        z_scales = keep.tile([P, N_NODES // K_PASS, N_OUT], U8, align_bytes=64)
+        with tc.tile_pool(name="zstage", bufs=2) as zstage, tc.tile_pool(name="zkeep", bufs=1) as zkeep:
+            w_raw = zkeep.tile([P, PACK, N_OUT], BF16)
+            for u in range(2):
+                nc.sync.dma_start(
+                    out=w_raw[:, 2 * u : 2 * u + 2, :],
+                    in_=Wout[256 * u : 256 * (u + 1), :].rearrange("(p e) o -> p e o", e=2),
+                )
+            bias_bc = zkeep.tile([P, N_OUT], BF16)
+            nc.sync.dma_start(out=bias_bc[:], in_=bout.partition_broadcast(P))
+            w_grouped = zkeep.tile([P, N_OUT, PACK], BF16, align_bytes=64)
+            nc.vector.tensor_copy(out=w_grouped[:], in_=w_raw[:].rearrange("p t o -> p o t"))
+            w_codes = zkeep.tile([P, N_OUT], U32, align_bytes=64)
+            w_scales = zkeep.tile([P, N_OUT], U8, align_bytes=64)
+            nc.vector.quantize_mx(
+                out=w_codes[:].bitcast(FP8X4),
+                scales=w_scales[:],
+                in_=w_grouped[:].rearrange("p o t -> p (o t)"),
+            )
+
+            z_grouped = zkeep.tile([P, N_NODES // K_PASS, N_OUT, PACK], BF16, align_bytes=64)
+            for c in range(GROUPS):
+                hn = zstage.tile([P, GROUP_TILES * N_FEAT], BF16)
+                nc.sync.dma_start(
+                    out=hn[:].rearrange("m (n f) -> m n f", f=N_FEAT),
+                    in_=Hn[c * GROUP_TILES * P : (c + 1) * GROUP_TILES * P, :].rearrange(
+                        "(n m) f -> m n f", m=P
+                    ),
+                )
+                hn_words = hn[:].bitcast(F32)
+                h_grouped = zstage.tile([P, GROUP_TILES * K_PASS], BF16, align_bytes=64)
+                h_grouped_words = h_grouped[:].bitcast(F32).rearrange(
+                    "p (n m u) -> p n m u", m=P, u=2
+                )
+                for pair in range(GROUP_TILES // 2):
+                    h_ps = psum_t.tile([P, 2, 2, P], F32, tag="tp")
+                    for a in range(2):
+                        for u in range(2):
+                            first = (2 * pair + a) * (N_FEAT // 2) + u * P
+                            nc.tensor.transpose(
+                                h_ps[:, a, u, :], hn_words[:, first : first + P], ident_f[:]
+                            )
+                    nc.scalar.copy(
+                        out=h_grouped_words[:, 2 * pair : 2 * pair + 2, :, :],
+                        in_=h_ps[:].rearrange("p a u m -> p a m u"),
+                    )
+                h_codes = zstage.tile([P, GROUP_TILES, P], U32, align_bytes=64)
+                h_scales = zstage.tile([P, GROUP_TILES, P], U8, align_bytes=64)
+                nc.vector.quantize_mx(
+                    out=h_codes[:].rearrange("p n m -> p (n m)").bitcast(FP8X4),
+                    scales=h_scales[:].rearrange("p n m -> p (n m)"),
+                    in_=h_grouped[:],
+                )
+                for half in range(GROUP_TILES // PACK):
+                    g = c * (GROUP_TILES // PACK) + half
+                    z_ps = psum_acc.tile([P, PACK, N_OUT], F32, tag="acc")
+                    for t in range(PACK):
+                        n = half * PACK + t
+                        nc.tensor.matmul_mx(
+                            out=z_ps[:, t, :],
+                            lhsT=h_codes[:, n, :].bitcast(FP8X4),
+                            lhsT_scale=h_scales[:, n, :],
+                            rhs=w_codes[:].bitcast(FP8X4),
+                            rhs_scale=w_scales[:],
+                            start=True,
+                            stop=True,
+                        )
+                    nc.vector.tensor_tensor(
+                        out=z_grouped[:, g, :, :],
+                        in0=z_ps[:].rearrange("p t o -> p o t"),
+                        in1=bias_bc[:].unsqueeze(2).to_broadcast([P, N_OUT, PACK]),
+                        op=ALU.add,
+                    )
+            nc.vector.quantize_mx(
+                out=z_codes[:].rearrange("p g o -> p (g o)").bitcast(FP8X4),
+                scales=z_scales[:].rearrange("p g o -> p (g o)"),
+                in_=z_grouped[:].rearrange("p g o t -> p (g o t)"),
+            )
+
+        d_rows = keep.tile([P, ROW_TILES], F32)
+        d_cols = keep.tile([P, N_NODES], F32)
+        sums_v = keep.tile([P, UNITS], F32)
+        sums_s = keep.tile([P, UNITS], F32)
+
+        def load_unit(unit):
+            r, h = divmod(unit, 2)
+            x = xpool.tile([P, HALF], BF16)
+            nc.sync.dma_start(out=x[:], in_=A1[r * P : (r + 1) * P, h * HALF : (h + 1) * HALF])
+            return x
+
+        with tc.tile_pool(name="sumpool", bufs=1) as sumpool, tc.tile_pool(name="dpool", bufs=2) as dpool:
+            junk_v = sumpool.tile([P, VECTOR_SUM_COLS], BF16)
+            junk_s = sumpool.tile([P, HALF - VECTOR_SUM_COLS], BF16)
+            for q in range(GROUPS):
+                units = slice(q * 2 * GROUP_TILES, (q + 1) * 2 * GROUP_TILES)
+                tiles = slice(q * GROUP_TILES, (q + 1) * GROUP_TILES)
+                for unit in range(q * 2 * GROUP_TILES, (q + 1) * 2 * GROUP_TILES):
+                    x = load_unit(unit)
+                    nc.vector.tensor_scalar(
+                        out=junk_v[:],
+                        in0=x[:, :VECTOR_SUM_COLS],
+                        scalar1=1.0,
+                        scalar2=None,
+                        op0=ALU.mult,
+                        op1=ALU.add,
+                        accum_out=sums_v[:, unit : unit + 1],
+                    )
+                    nc.scalar.activation(
+                        out=junk_s[:],
+                        in_=x[:, VECTOR_SUM_COLS:],
+                        func=ACT.Copy,
+                        accum_out=sums_s[:, unit : unit + 1],
+                    )
+                part = dpool.tile([P, GROUP_TILES, 2], F32)
+                nc.vector.tensor_tensor(
+                    out=part[:].rearrange("p r h -> p (r h)"),
+                    in0=sums_v[:, units],
+                    in1=sums_s[:, units],
+                    op=ALU.add,
+                )
+                rowsum = dpool.tile([P, GROUP_TILES], F32)
+                nc.vector.tensor_tensor(
+                    out=rowsum[:], in0=part[:, :, 0], in1=part[:, :, 1], op=ALU.add
+                )
+                root = dpool.tile([P, GROUP_TILES], F32)
+                nc.scalar.sqrt(root[:], rowsum[:])
+                guess = dpool.tile([P, GROUP_TILES], F32)
+                nc.vector.reciprocal(guess[:], root[:])
+                corr = dpool.tile([P, GROUP_TILES], F32)
+                nc.vector.tensor_tensor(out=corr[:], in0=guess[:], in1=guess[:], op=ALU.mult)
+                nc.vector.tensor_tensor(out=corr[:], in0=corr[:], in1=rowsum[:], op=ALU.mult)
+                nc.vector.tensor_scalar(
+                    out=corr[:], in0=corr[:], scalar1=-0.5, scalar2=1.5, op0=ALU.mult, op1=ALU.add
+                )
+                nc.vector.tensor_tensor(
+                    out=d_rows[:, tiles], in0=guess[:], in1=corr[:], op=ALU.mult
+                )
+                repeated = dpool.tile([P, GROUP_TILES, P], F32)
+                nc.vector.tensor_copy(
+                    out=repeated[:],
+                    in_=d_rows[:, tiles].unsqueeze(2).to_broadcast([P, GROUP_TILES, P]),
+                )
+                for bank in range(GROUP_TILES // TILES_PER_BANK):
+                    d_ps = psum_t.tile([P, TILES_PER_BANK, P], F32, tag="tp")
+                    for a in range(TILES_PER_BANK):
+                        nc.tensor.transpose(
+                            d_ps[:, a, :], repeated[:, bank * TILES_PER_BANK + a, :], ident_f[:]
+                        )
+                    first = (q * GROUP_TILES + bank * TILES_PER_BANK) * P
+                    nc.scalar.copy(
+                        out=d_cols[:, first : first + TILES_PER_BANK * P],
+                        in_=d_ps[:].rearrange("p a n -> p (a n)"),
+                    )
+
+        work = ctx.enter_context(tc.tile_pool(name="work", bufs=LAG + 2))
+        ypool = ctx.enter_context(tc.tile_pool(name="ypool", bufs=2))
+        out_tiles = out.rearrange("(r p) o -> p r o", p=P)
+
+        def scale_and_transpose(unit):
+            r, h = divmod(unit, 2)
+            x = load_unit(unit)
+            a_hat = work.tile([P, HALF], BF16)
+            nc.vector.scalar_tensor_tensor(
+                out=a_hat[:],
+                in0=x[:],
+                scalar=d_rows[:, r : r + 1],
+                in1=d_cols[:, h * HALF : (h + 1) * HALF],
+                op0=ALU.mult,
+                op1=ALU.mult,
+            )
+            grouped = work.tile([P, PASSES_PER_UNIT, P, PACK], BF16, align_bytes=64)
+            for g in range(PASSES_PER_UNIT):
+                a_ps = psum_t.tile([P, PACK, P], BF16, tag="tp")
+                for t in range(PACK):
+                    first = (g * PACK + t) * P
+                    nc.tensor.transpose(a_ps[:, t, :], a_hat[:, first : first + P], ident_bf[:])
+                nc.scalar.copy(out=grouped[:, g, :, :], in_=a_ps[:].rearrange("p t i -> p i t"))
+            return grouped
+
+        def quantise_and_multiply(unit, grouped, y_ps):
+            r, h = divmod(unit, 2)
+            a_codes = work.tile([P, PASSES_PER_UNIT, P], U32, align_bytes=64)
+            a_scales = work.tile([P, PASSES_PER_UNIT, P], U8, align_bytes=64)
+            nc.vector.quantize_mx(
+                out=a_codes[:].rearrange("p g i -> p (g i)").bitcast(FP8X4),
+                scales=a_scales[:].rearrange("p g i -> p (g i)"),
+                in_=grouped[:].rearrange("p g i t -> p (g i t)"),
+            )
+            for g in range(PASSES_PER_UNIT):
+                z_pass = h * PASSES_PER_UNIT + g
+                nc.tensor.matmul_mx(
+                    out=y_ps[:, r % TILES_PER_BANK, :],
+                    lhsT=a_codes[:, g, :].bitcast(FP8X4),
+                    lhsT_scale=a_scales[:, g, :],
+                    rhs=z_codes[:, z_pass, :].bitcast(FP8X4),
+                    rhs_scale=z_scales[:, z_pass, :],
+                    start=(z_pass == 0),
+                    stop=(z_pass == N_NODES // K_PASS - 1),
+                )
+
+        def leaky_relu_and_store(first_tile, y_ps):
+            y_sb = ypool.tile([P, TILES_PER_BANK, N_OUT], F32)
+            nc.scalar.copy(out=y_sb[:], in_=y_ps[:])
+            result = ypool.tile([P, TILES_PER_BANK, N_OUT], F32)
+            nc.vector.scalar_tensor_tensor(
+                out=result[:].rearrange("p r o -> p (r o)"),
+                in0=y_ps[:].rearrange("p r o -> p (r o)"),
+                scalar=LEAKY_SLOPE,
+                in1=y_sb[:].rearrange("p r o -> p (r o)"),
+                op0=ALU.mult,
+                op1=ALU.max,
+            )
+            nc.sync.dma_start(
+                out=out_tiles[:, first_tile : first_tile + TILES_PER_BANK, :], in_=result[:]
+            )
+
+        waiting = []
+        y_ps = None
+        for step in range(UNITS + LAG):
+            if step < UNITS:
+                waiting.append(scale_and_transpose(step))
+            unit = step - LAG
+            if unit >= 0:
+                if unit % (2 * TILES_PER_BANK) == 0:
+                    y_ps = psum_acc.tile([P, TILES_PER_BANK, N_OUT], F32, tag="acc")
+                quantise_and_multiply(unit, waiting[unit], y_ps)
+                if unit % (2 * TILES_PER_BANK) == 2 * TILES_PER_BANK - 1:
+                    leaky_relu_and_store(unit // 2 - (TILES_PER_BANK - 1), y_ps)

@@ -20,14 +20,19 @@ N_OUT = 128
 LEAKY_SLOPE = 0.01
 
 ROW_TILES = N_NODES // P
+PASSES = N_NODES // K_PASS
 HALF = N_NODES // 2
 PASSES_PER_UNIT = HALF // K_PASS
 UNITS = 2 * ROW_TILES
 GROUP_TILES = 8
 GROUPS = ROW_TILES // GROUP_TILES
-VECTOR_SUM_COLS = 1344
-LAG = 2
+VECTOR_SUM_COLS = 2688
 TILES_PER_BANK = 4
+UNITS_PER_BANK = 2 * TILES_PER_BANK
+PREFETCH = 4
+QUANT_LAG = 4
+MATMUL_LAG = QUANT_LAG + 1
+STORE_LAG = MATMUL_LAG + 3
 
 FLOPS = 2 * N_NODES * N_FEAT * N_OUT + 2 * N_NODES * N_NODES * N_OUT
 
@@ -36,9 +41,9 @@ def tile_gcnlayer_pb_t_kernel(tc, A1, Hn, Wout, bout, out):
     nc = tc.nc
     with ExitStack() as ctx:
         keep = ctx.enter_context(tc.tile_pool(name="keep", bufs=1))
-        xpool = ctx.enter_context(tc.tile_pool(name="xpool", bufs=6))
-        psum_t = ctx.enter_context(tc.psum_pool(name="psum_t", bufs=5))
-        psum_acc = ctx.enter_context(tc.psum_pool(name="psum_acc", bufs=3))
+        xpool = ctx.enter_context(tc.tile_pool(name="xpool", bufs=PREFETCH + 2))
+        psum_t = ctx.enter_context(tc.psum_pool(name="psum_t", bufs=6))
+        psum_acc = ctx.enter_context(tc.psum_pool(name="psum_acc", bufs=2))
 
         ident_bf = keep.tile([P, P], BF16)
         make_identity(nc, ident_bf[:])
@@ -50,8 +55,8 @@ def tile_gcnlayer_pb_t_kernel(tc, A1, Hn, Wout, bout, out):
         warm = keep.tile([P, 1], F32)
         nc.scalar.sqrt(warm[:], one[:])
 
-        z_codes = keep.tile([P, N_NODES // K_PASS, N_OUT], U32, align_bytes=64)
-        z_scales = keep.tile([P, N_NODES // K_PASS, N_OUT], U8, align_bytes=64)
+        z_codes = keep.tile([P, PASSES, N_OUT], U32, align_bytes=64)
+        z_scales = keep.tile([P, PASSES, N_OUT], U8, align_bytes=64)
         with tc.tile_pool(name="zstage", bufs=2) as zstage, tc.tile_pool(name="zkeep", bufs=1) as zkeep:
             w_raw = zkeep.tile([P, PACK, N_OUT], BF16)
             for u in range(2):
@@ -71,7 +76,7 @@ def tile_gcnlayer_pb_t_kernel(tc, A1, Hn, Wout, bout, out):
                 in_=w_grouped[:].rearrange("p o t -> p (o t)"),
             )
 
-            z_grouped = zkeep.tile([P, N_NODES // K_PASS, N_OUT, PACK], BF16, align_bytes=64)
+            z_grouped = zkeep.tile([P, PASSES, N_OUT, PACK], BF16, align_bytes=64)
             for c in range(GROUPS):
                 hn = zstage.tile([P, GROUP_TILES * N_FEAT], BF16)
                 nc.sync.dma_start(
@@ -132,86 +137,92 @@ def tile_gcnlayer_pb_t_kernel(tc, A1, Hn, Wout, bout, out):
 
         d_rows = keep.tile([P, ROW_TILES], F32)
         d_cols = keep.tile([P, N_NODES], F32)
-        sums_v = keep.tile([P, UNITS], F32)
-        sums_s = keep.tile([P, UNITS], F32)
+        sums_v = keep.tile([P, ROW_TILES], F32)
+        sums_s = keep.tile([P, ROW_TILES], F32)
+        dpool = ctx.enter_context(tc.tile_pool(name="dpool", bufs=2))
 
-        def load_unit(unit):
-            r, h = divmod(unit, 2)
-            x = xpool.tile([P, HALF], BF16)
-            nc.sync.dma_start(out=x[:], in_=A1[r * P : (r + 1) * P, h * HALF : (h + 1) * HALF])
-            return x
+        def begin_d(q):
+            tiles = slice(q * GROUP_TILES, (q + 1) * GROUP_TILES)
+            rowsum = dpool.tile([P, GROUP_TILES], F32)
+            nc.vector.tensor_tensor(
+                out=rowsum[:], in0=sums_v[:, tiles], in1=sums_s[:, tiles], op=ALU.add
+            )
+            root = dpool.tile([P, GROUP_TILES], F32)
+            nc.scalar.sqrt(root[:], rowsum[:])
+            return rowsum, root
 
-        with tc.tile_pool(name="sumpool", bufs=1) as sumpool, tc.tile_pool(name="dpool", bufs=2) as dpool:
+        def finish_d(q, rowsum, root):
+            tiles = slice(q * GROUP_TILES, (q + 1) * GROUP_TILES)
+            guess = dpool.tile([P, GROUP_TILES], F32)
+            nc.vector.reciprocal(guess[:], root[:])
+            corr = dpool.tile([P, GROUP_TILES], F32)
+            nc.vector.tensor_tensor(out=corr[:], in0=guess[:], in1=guess[:], op=ALU.mult)
+            nc.vector.tensor_tensor(out=corr[:], in0=corr[:], in1=rowsum[:], op=ALU.mult)
+            nc.vector.tensor_scalar(
+                out=corr[:], in0=corr[:], scalar1=-0.5, scalar2=1.5, op0=ALU.mult, op1=ALU.add
+            )
+            nc.vector.tensor_tensor(out=d_rows[:, tiles], in0=guess[:], in1=corr[:], op=ALU.mult)
+            repeated = dpool.tile([P, GROUP_TILES, P], F32)
+            nc.vector.tensor_copy(
+                out=repeated[:],
+                in_=d_rows[:, tiles].unsqueeze(2).to_broadcast([P, GROUP_TILES, P]),
+            )
+            for bank in range(GROUP_TILES // TILES_PER_BANK):
+                d_ps = psum_t.tile([P, TILES_PER_BANK, P], F32, tag="tp")
+                for a in range(TILES_PER_BANK):
+                    nc.tensor.transpose(
+                        d_ps[:, a, :], repeated[:, bank * TILES_PER_BANK + a, :], ident_f[:]
+                    )
+                first = (q * GROUP_TILES + bank * TILES_PER_BANK) * P
+                nc.scalar.copy(
+                    out=d_cols[:, first : first + TILES_PER_BANK * P],
+                    in_=d_ps[:].rearrange("p a n -> p (a n)"),
+                )
+
+        with tc.tile_pool(name="rowpool", bufs=4) as rowpool, tc.tile_pool(name="sumpool", bufs=1) as sumpool:
             junk_v = sumpool.tile([P, VECTOR_SUM_COLS], BF16)
-            junk_s = sumpool.tile([P, HALF - VECTOR_SUM_COLS], BF16)
+            junk_s = sumpool.tile([P, N_NODES - VECTOR_SUM_COLS], BF16)
             for q in range(GROUPS):
-                units = slice(q * 2 * GROUP_TILES, (q + 1) * 2 * GROUP_TILES)
-                tiles = slice(q * GROUP_TILES, (q + 1) * GROUP_TILES)
-                for unit in range(q * 2 * GROUP_TILES, (q + 1) * 2 * GROUP_TILES):
-                    x = load_unit(unit)
+                for r in range(q * GROUP_TILES, (q + 1) * GROUP_TILES):
+                    rows = rowpool.tile([P, N_NODES], BF16)
+                    nc.sync.dma_start(out=rows[:], in_=A1[r * P : (r + 1) * P, :])
                     nc.vector.tensor_scalar(
                         out=junk_v[:],
-                        in0=x[:, :VECTOR_SUM_COLS],
+                        in0=rows[:, :VECTOR_SUM_COLS],
                         scalar1=1.0,
                         scalar2=None,
                         op0=ALU.mult,
                         op1=ALU.add,
-                        accum_out=sums_v[:, unit : unit + 1],
+                        accum_out=sums_v[:, r : r + 1],
                     )
                     nc.scalar.activation(
                         out=junk_s[:],
-                        in_=x[:, VECTOR_SUM_COLS:],
+                        in_=rows[:, VECTOR_SUM_COLS:],
                         func=ACT.Copy,
-                        accum_out=sums_s[:, unit : unit + 1],
+                        accum_out=sums_s[:, r : r + 1],
                     )
-                part = dpool.tile([P, GROUP_TILES, 2], F32)
-                nc.vector.tensor_tensor(
-                    out=part[:].rearrange("p r h -> p (r h)"),
-                    in0=sums_v[:, units],
-                    in1=sums_s[:, units],
-                    op=ALU.add,
-                )
-                rowsum = dpool.tile([P, GROUP_TILES], F32)
-                nc.vector.tensor_tensor(
-                    out=rowsum[:], in0=part[:, :, 0], in1=part[:, :, 1], op=ALU.add
-                )
-                root = dpool.tile([P, GROUP_TILES], F32)
-                nc.scalar.sqrt(root[:], rowsum[:])
-                guess = dpool.tile([P, GROUP_TILES], F32)
-                nc.vector.reciprocal(guess[:], root[:])
-                corr = dpool.tile([P, GROUP_TILES], F32)
-                nc.vector.tensor_tensor(out=corr[:], in0=guess[:], in1=guess[:], op=ALU.mult)
-                nc.vector.tensor_tensor(out=corr[:], in0=corr[:], in1=rowsum[:], op=ALU.mult)
-                nc.vector.tensor_scalar(
-                    out=corr[:], in0=corr[:], scalar1=-0.5, scalar2=1.5, op0=ALU.mult, op1=ALU.add
-                )
-                nc.vector.tensor_tensor(
-                    out=d_rows[:, tiles], in0=guess[:], in1=corr[:], op=ALU.mult
-                )
-                repeated = dpool.tile([P, GROUP_TILES, P], F32)
-                nc.vector.tensor_copy(
-                    out=repeated[:],
-                    in_=d_rows[:, tiles].unsqueeze(2).to_broadcast([P, GROUP_TILES, P]),
-                )
-                for bank in range(GROUP_TILES // TILES_PER_BANK):
-                    d_ps = psum_t.tile([P, TILES_PER_BANK, P], F32, tag="tp")
-                    for a in range(TILES_PER_BANK):
-                        nc.tensor.transpose(
-                            d_ps[:, a, :], repeated[:, bank * TILES_PER_BANK + a, :], ident_f[:]
-                        )
-                    first = (q * GROUP_TILES + bank * TILES_PER_BANK) * P
-                    nc.scalar.copy(
-                        out=d_cols[:, first : first + TILES_PER_BANK * P],
-                        in_=d_ps[:].rearrange("p a n -> p (a n)"),
-                    )
+                rowsum, root = begin_d(q)
+                if q < GROUPS - 1:
+                    finish_d(q, rowsum, root)
 
-        work = ctx.enter_context(tc.tile_pool(name="work", bufs=LAG + 2))
+        work = ctx.enter_context(tc.tile_pool(name="work", bufs=QUANT_LAG + 2))
+        codes_pool = ctx.enter_context(tc.tile_pool(name="codes_pool", bufs=2))
         ypool = ctx.enter_context(tc.tile_pool(name="ypool", bufs=2))
         out_tiles = out.rearrange("(r p) o -> p r o", p=P)
 
-        def scale_and_transpose(unit):
-            r, h = divmod(unit, 2)
-            x = load_unit(unit)
+        def row_tile_and_half(unit):
+            bank, within = divmod(unit, UNITS_PER_BANK)
+            h, k = divmod(within, TILES_PER_BANK)
+            return bank * TILES_PER_BANK + k, h
+
+        def load_unit(unit):
+            r, h = row_tile_and_half(unit)
+            x = xpool.tile([P, HALF], BF16)
+            nc.sync.dma_start(out=x[:], in_=A1[r * P : (r + 1) * P, h * HALF : (h + 1) * HALF])
+            return x
+
+        def scale_and_transpose(unit, x):
+            r, h = row_tile_and_half(unit)
             a_hat = work.tile([P, HALF], BF16)
             nc.vector.scalar_tensor_tensor(
                 out=a_hat[:],
@@ -230,30 +241,34 @@ def tile_gcnlayer_pb_t_kernel(tc, A1, Hn, Wout, bout, out):
                 nc.scalar.copy(out=grouped[:, g, :, :], in_=a_ps[:].rearrange("p t i -> p i t"))
             return grouped
 
-        def quantise_and_multiply(unit, grouped, y_ps):
-            r, h = divmod(unit, 2)
-            a_codes = work.tile([P, PASSES_PER_UNIT, P], U32, align_bytes=64)
-            a_scales = work.tile([P, PASSES_PER_UNIT, P], U8, align_bytes=64)
+        def quantise(unit, grouped, a_codes, a_scales):
+            within = unit % UNITS_PER_BANK
             nc.vector.quantize_mx(
-                out=a_codes[:].rearrange("p g i -> p (g i)").bitcast(FP8X4),
-                scales=a_scales[:].rearrange("p g i -> p (g i)"),
+                out=a_codes[:, within, :, :].rearrange("p g i -> p (g i)").bitcast(FP8X4),
+                scales=a_scales[:, within, :, :].rearrange("p g i -> p (g i)"),
                 in_=grouped[:].rearrange("p g i t -> p (g i t)"),
             )
-            for g in range(PASSES_PER_UNIT):
-                z_pass = h * PASSES_PER_UNIT + g
-                nc.tensor.matmul_mx(
-                    out=y_ps[:, r % TILES_PER_BANK, :],
-                    lhsT=a_codes[:, g, :].bitcast(FP8X4),
-                    lhsT_scale=a_scales[:, g, :],
-                    rhs=z_codes[:, z_pass, :].bitcast(FP8X4),
-                    rhs_scale=z_scales[:, z_pass, :],
-                    start=(z_pass == 0),
-                    stop=(z_pass == N_NODES // K_PASS - 1),
-                )
 
-        def leaky_relu_and_store(first_tile, y_ps):
+        def multiply_bank(a_codes, a_scales):
+            y_ps = psum_acc.tile([P, TILES_PER_BANK, N_OUT], F32, tag="acc")
+            for k in range(TILES_PER_BANK):
+                for z_pass in range(PASSES):
+                    h, g = divmod(z_pass, PASSES_PER_UNIT)
+                    within = h * TILES_PER_BANK + k
+                    nc.tensor.matmul_mx(
+                        out=y_ps[:, k, :],
+                        lhsT=a_codes[:, within, g, :].bitcast(FP8X4),
+                        lhsT_scale=a_scales[:, within, g, :],
+                        rhs=z_codes[:, z_pass, :].bitcast(FP8X4),
+                        rhs_scale=z_scales[:, z_pass, :],
+                        start=(z_pass == 0),
+                        stop=(z_pass == PASSES - 1),
+                    )
             y_sb = ypool.tile([P, TILES_PER_BANK, N_OUT], F32)
             nc.scalar.copy(out=y_sb[:], in_=y_ps[:])
+            return y_ps, y_sb
+
+        def leaky_relu_and_store(bank, y_ps, y_sb):
             result = ypool.tile([P, TILES_PER_BANK, N_OUT], F32)
             nc.vector.scalar_tensor_tensor(
                 out=result[:].rearrange("p r o -> p (r o)"),
@@ -263,19 +278,36 @@ def tile_gcnlayer_pb_t_kernel(tc, A1, Hn, Wout, bout, out):
                 op0=ALU.mult,
                 op1=ALU.max,
             )
+            first_tile = bank * TILES_PER_BANK
             nc.sync.dma_start(
                 out=out_tiles[:, first_tile : first_tile + TILES_PER_BANK, :], in_=result[:]
             )
 
-        waiting = []
-        y_ps = None
-        for step in range(UNITS + LAG):
-            if step < UNITS:
-                waiting.append(scale_and_transpose(step))
-            unit = step - LAG
-            if unit >= 0:
-                if unit % (2 * TILES_PER_BANK) == 0:
-                    y_ps = psum_acc.tile([P, TILES_PER_BANK, N_OUT], F32, tag="acc")
-                quantise_and_multiply(unit, waiting[unit], y_ps)
-                if unit % (2 * TILES_PER_BANK) == 2 * TILES_PER_BANK - 1:
-                    leaky_relu_and_store(unit // 2 - (TILES_PER_BANK - 1), y_ps)
+        bank_shape = [P, UNITS_PER_BANK, PASSES_PER_UNIT, P]
+        x_tiles = []
+        grouped_tiles = []
+        code_tiles = []
+        sum_tiles = []
+        for unit in range(PREFETCH):
+            x_tiles.append(load_unit(unit))
+        with tc.manual_schedule():
+            for step in range(UNITS + STORE_LAG):
+                if step + PREFETCH < UNITS:
+                    x_tiles.append(load_unit(step + PREFETCH))
+                if step < UNITS:
+                    grouped_tiles.append(scale_and_transpose(step, x_tiles[step]))
+                if step == 0:
+                    finish_d(GROUPS - 1, rowsum, root)
+                unit = step - QUANT_LAG
+                if 0 <= unit < UNITS:
+                    if unit % UNITS_PER_BANK == 0:
+                        a_codes = codes_pool.tile(bank_shape, U32, align_bytes=64)
+                        a_scales = codes_pool.tile(bank_shape, U8, align_bytes=64)
+                        code_tiles.append((a_codes, a_scales))
+                    quantise(unit, grouped_tiles[unit], a_codes, a_scales)
+                bank, within = divmod(step - MATMUL_LAG, UNITS_PER_BANK)
+                if bank >= 0 and within == UNITS_PER_BANK - 1:
+                    sum_tiles.append(multiply_bank(code_tiles[bank][0], code_tiles[bank][1]))
+                bank, within = divmod(step - STORE_LAG, UNITS_PER_BANK)
+                if bank >= 0 and within == UNITS_PER_BANK - 1:
+                    leaky_relu_and_store(bank, sum_tiles[bank][0], sum_tiles[bank][1])

@@ -29,9 +29,13 @@ GROUPS = ROW_TILES // GROUP_TILES
 VECTOR_SUM_COLS = 2688
 TILES_PER_BANK = 4
 UNITS_PER_BANK = 2 * TILES_PER_BANK
+BANKS = ROW_TILES // TILES_PER_BANK
+EARLY_UNITS = TILES_PER_BANK
+EARLY_EVERY = 4
 PREFETCH = 4
 QUANT_LAG = 4
 MATMUL_LAG = QUANT_LAG + 1
+TILES_PER_RUN = 2
 STORE_LAG = MATMUL_LAG + 3
 
 FLOPS = 2 * N_NODES * N_FEAT * N_OUT + 2 * N_NODES * N_NODES * N_OUT
@@ -44,6 +48,10 @@ def tile_gcnlayer_pb_t_kernel(tc, A1, Hn, Wout, bout, out):
         xpool = ctx.enter_context(tc.tile_pool(name="xpool", bufs=PREFETCH + 2))
         psum_t = ctx.enter_context(tc.psum_pool(name="psum_t", bufs=6))
         psum_acc = ctx.enter_context(tc.psum_pool(name="psum_acc", bufs=2))
+        dpool = ctx.enter_context(tc.tile_pool(name="dpool", bufs=2))
+        kept = ctx.enter_context(tc.tile_pool(name="kept", bufs=EARLY_UNITS))
+        hat_pool = ctx.enter_context(tc.tile_pool(name="hat_pool", bufs=3))
+        grouped_pool = ctx.enter_context(tc.tile_pool(name="grouped_pool", bufs=QUANT_LAG + 2))
 
         ident_bf = keep.tile([P, P], BF16)
         make_identity(nc, ident_bf[:])
@@ -139,7 +147,6 @@ def tile_gcnlayer_pb_t_kernel(tc, A1, Hn, Wout, bout, out):
         d_cols = keep.tile([P, N_NODES], F32)
         sums_v = keep.tile([P, ROW_TILES], F32)
         sums_s = keep.tile([P, ROW_TILES], F32)
-        dpool = ctx.enter_context(tc.tile_pool(name="dpool", bufs=2))
 
         def begin_d(q):
             tiles = slice(q * GROUP_TILES, (q + 1) * GROUP_TILES)
@@ -179,12 +186,62 @@ def tile_gcnlayer_pb_t_kernel(tc, A1, Hn, Wout, bout, out):
                     in_=d_ps[:].rearrange("p a n -> p (a n)"),
                 )
 
-        with tc.tile_pool(name="rowpool", bufs=4) as rowpool, tc.tile_pool(name="sumpool", bufs=1) as sumpool:
+        def half_bank(bank, h):
+            return [(bank, h * TILES_PER_BANK + k) for k in range(TILES_PER_BANK)]
+
+        order = half_bank(0, 0)
+        for bank in range(BANKS):
+            if bank + 1 < BANKS:
+                order.extend(half_bank(bank + 1, 0))
+            order.extend(half_bank(bank, 1))
+
+        def row_tile_and_half(unit):
+            bank, within = unit
+            h, k = divmod(within, TILES_PER_BANK)
+            return bank * TILES_PER_BANK + k, h
+
+        kept_rows = []
+
+        def fetch_unit(unit):
+            r, h = row_tile_and_half(unit)
+            if r < len(kept_rows):
+                return kept_rows[r][:, h * HALF : (h + 1) * HALF]
+            x = xpool.tile([P, HALF], BF16)
+            nc.sync.dma_start(out=x[:], in_=A1[r * P : (r + 1) * P, h * HALF : (h + 1) * HALF])
+            return x[:]
+
+        def scale_and_transpose(unit, x):
+            r, h = row_tile_and_half(unit)
+            a_hat = hat_pool.tile([P, HALF], BF16)
+            nc.vector.scalar_tensor_tensor(
+                out=a_hat[:],
+                in0=x,
+                scalar=d_rows[:, r : r + 1],
+                in1=d_cols[:, h * HALF : (h + 1) * HALF],
+                op0=ALU.mult,
+                op1=ALU.mult,
+            )
+            grouped = grouped_pool.tile([P, PASSES_PER_UNIT, P, PACK], BF16, align_bytes=64)
+            for g in range(PASSES_PER_UNIT):
+                a_ps = psum_t.tile([P, PACK, P], BF16, tag="tp")
+                for t in range(PACK):
+                    first = (g * PACK + t) * P
+                    nc.tensor.transpose(a_ps[:, t, :], a_hat[:, first : first + P], ident_bf[:])
+                nc.scalar.copy(out=grouped[:, g, :, :], in_=a_ps[:].rearrange("p t i -> p i t"))
+            return grouped
+
+        grouped_tiles = []
+
+        with tc.tile_pool(name="rowpool", bufs=5) as rowpool, tc.tile_pool(name="sumpool", bufs=1) as sumpool:
             junk_v = sumpool.tile([P, VECTOR_SUM_COLS], BF16)
             junk_s = sumpool.tile([P, N_NODES - VECTOR_SUM_COLS], BF16)
             for q in range(GROUPS):
                 for r in range(q * GROUP_TILES, (q + 1) * GROUP_TILES):
-                    rows = rowpool.tile([P, N_NODES], BF16)
+                    if r < EARLY_UNITS:
+                        rows = kept.tile([P, N_NODES], BF16)
+                        kept_rows.append(rows)
+                    else:
+                        rows = rowpool.tile([P, N_NODES], BF16)
                     nc.sync.dma_start(out=rows[:], in_=A1[r * P : (r + 1) * P, :])
                     nc.vector.tensor_scalar(
                         out=junk_v[:],
@@ -201,74 +258,44 @@ def tile_gcnlayer_pb_t_kernel(tc, A1, Hn, Wout, bout, out):
                         func=ACT.Copy,
                         accum_out=sums_s[:, r : r + 1],
                     )
+                    if r >= ROW_TILES // 2 and r % EARLY_EVERY == 0:
+                        unit = order[len(grouped_tiles)]
+                        grouped_tiles.append(scale_and_transpose(unit, fetch_unit(unit)))
                 rowsum, root = begin_d(q)
                 if q < GROUPS - 1:
                     finish_d(q, rowsum, root)
 
-        work = ctx.enter_context(tc.tile_pool(name="work", bufs=QUANT_LAG + 2))
-        codes_pool = ctx.enter_context(tc.tile_pool(name="codes_pool", bufs=2))
+        codes_pool = ctx.enter_context(tc.tile_pool(name="codes_pool", bufs=3))
         ypool = ctx.enter_context(tc.tile_pool(name="ypool", bufs=2))
         out_tiles = out.rearrange("(r p) o -> p r o", p=P)
+        bank_shape = [P, UNITS_PER_BANK, PASSES_PER_UNIT, P]
 
-        def row_tile_and_half(unit):
-            bank, within = divmod(unit, UNITS_PER_BANK)
-            h, k = divmod(within, TILES_PER_BANK)
-            return bank * TILES_PER_BANK + k, h
-
-        def load_unit(unit):
-            r, h = row_tile_and_half(unit)
-            x = xpool.tile([P, HALF], BF16)
-            nc.sync.dma_start(out=x[:], in_=A1[r * P : (r + 1) * P, h * HALF : (h + 1) * HALF])
-            return x
-
-        def scale_and_transpose(unit, x):
-            r, h = row_tile_and_half(unit)
-            a_hat = work.tile([P, HALF], BF16)
-            nc.vector.scalar_tensor_tensor(
-                out=a_hat[:],
-                in0=x[:],
-                scalar=d_rows[:, r : r + 1],
-                in1=d_cols[:, h * HALF : (h + 1) * HALF],
-                op0=ALU.mult,
-                op1=ALU.mult,
-            )
-            grouped = work.tile([P, PASSES_PER_UNIT, P, PACK], BF16, align_bytes=64)
-            for g in range(PASSES_PER_UNIT):
-                a_ps = psum_t.tile([P, PACK, P], BF16, tag="tp")
-                for t in range(PACK):
-                    first = (g * PACK + t) * P
-                    nc.tensor.transpose(a_ps[:, t, :], a_hat[:, first : first + P], ident_bf[:])
-                nc.scalar.copy(out=grouped[:, g, :, :], in_=a_ps[:].rearrange("p t i -> p i t"))
-            return grouped
-
-        def quantise(unit, grouped, a_codes, a_scales):
-            within = unit % UNITS_PER_BANK
+        def quantise(unit, grouped):
+            bank, within = unit
+            a_codes, a_scales = code_tiles[bank]
             nc.vector.quantize_mx(
                 out=a_codes[:, within, :, :].rearrange("p g i -> p (g i)").bitcast(FP8X4),
                 scales=a_scales[:, within, :, :].rearrange("p g i -> p (g i)"),
                 in_=grouped[:].rearrange("p g i t -> p (g i t)"),
             )
 
-        def multiply_bank(a_codes, a_scales):
-            y_ps = psum_acc.tile([P, TILES_PER_BANK, N_OUT], F32, tag="acc")
-            for k in range(TILES_PER_BANK):
-                for z_pass in range(PASSES):
-                    h, g = divmod(z_pass, PASSES_PER_UNIT)
-                    within = h * TILES_PER_BANK + k
-                    nc.tensor.matmul_mx(
-                        out=y_ps[:, k, :],
-                        lhsT=a_codes[:, within, g, :].bitcast(FP8X4),
-                        lhsT_scale=a_scales[:, within, g, :],
-                        rhs=z_codes[:, z_pass, :].bitcast(FP8X4),
-                        rhs_scale=z_scales[:, z_pass, :],
-                        start=(z_pass == 0),
-                        stop=(z_pass == PASSES - 1),
-                    )
-            y_sb = ypool.tile([P, TILES_PER_BANK, N_OUT], F32)
-            nc.scalar.copy(out=y_sb[:], in_=y_ps[:])
-            return y_ps, y_sb
+        def multiply_row_tile(bank, k):
+            a_codes, a_scales = code_tiles[bank]
+            for z_pass in range(PASSES):
+                h, g = divmod(z_pass, PASSES_PER_UNIT)
+                within = h * TILES_PER_BANK + k
+                nc.tensor.matmul_mx(
+                    out=sum_tiles[bank][:, k, :],
+                    lhsT=a_codes[:, within, g, :].bitcast(FP8X4),
+                    lhsT_scale=a_scales[:, within, g, :],
+                    rhs=z_codes[:, z_pass, :].bitcast(FP8X4),
+                    rhs_scale=z_scales[:, z_pass, :],
+                    start=(z_pass == 0),
+                    stop=(z_pass == PASSES - 1),
+                )
 
-        def leaky_relu_and_store(bank, y_ps, y_sb):
+        def leaky_relu_and_store(bank, y_sb):
+            y_ps = sum_tiles[bank]
             result = ypool.tile([P, TILES_PER_BANK, N_OUT], F32)
             nc.vector.scalar_tensor_tensor(
                 out=result[:].rearrange("p r o -> p (r o)"),
@@ -283,31 +310,41 @@ def tile_gcnlayer_pb_t_kernel(tc, A1, Hn, Wout, bout, out):
                 out=out_tiles[:, first_tile : first_tile + TILES_PER_BANK, :], in_=result[:]
             )
 
-        bank_shape = [P, UNITS_PER_BANK, PASSES_PER_UNIT, P]
-        x_tiles = []
-        grouped_tiles = []
         code_tiles = []
         sum_tiles = []
-        for unit in range(PREFETCH):
-            x_tiles.append(load_unit(unit))
+        copy_tiles = []
+        x_views = [None] * EARLY_UNITS
+        for step in range(EARLY_UNITS, EARLY_UNITS + PREFETCH):
+            x_views.append(fetch_unit(order[step]))
         with tc.manual_schedule():
-            for step in range(UNITS + STORE_LAG):
+            for step in range(EARLY_UNITS, UNITS + STORE_LAG):
                 if step + PREFETCH < UNITS:
-                    x_tiles.append(load_unit(step + PREFETCH))
+                    x_views.append(fetch_unit(order[step + PREFETCH]))
                 if step < UNITS:
-                    grouped_tiles.append(scale_and_transpose(step, x_tiles[step]))
-                if step == 0:
+                    grouped_tiles.append(scale_and_transpose(order[step], x_views[step]))
+                if step == EARLY_UNITS:
                     finish_d(GROUPS - 1, rowsum, root)
-                unit = step - QUANT_LAG
-                if 0 <= unit < UNITS:
-                    if unit % UNITS_PER_BANK == 0:
+                if 0 <= step - QUANT_LAG < UNITS:
+                    unit = order[step - QUANT_LAG]
+                    if unit[1] == 0:
                         a_codes = codes_pool.tile(bank_shape, U32, align_bytes=64)
                         a_scales = codes_pool.tile(bank_shape, U8, align_bytes=64)
                         code_tiles.append((a_codes, a_scales))
-                    quantise(unit, grouped_tiles[unit], a_codes, a_scales)
-                bank, within = divmod(step - MATMUL_LAG, UNITS_PER_BANK)
-                if bank >= 0 and within == UNITS_PER_BANK - 1:
-                    sum_tiles.append(multiply_bank(code_tiles[bank][0], code_tiles[bank][1]))
-                bank, within = divmod(step - STORE_LAG, UNITS_PER_BANK)
-                if bank >= 0 and within == UNITS_PER_BANK - 1:
-                    leaky_relu_and_store(bank, sum_tiles[bank][0], sum_tiles[bank][1])
+                    quantise(unit, grouped_tiles[step - QUANT_LAG])
+                if 0 <= step - MATMUL_LAG < UNITS:
+                    bank, within = order[step - MATMUL_LAG]
+                    k = within - TILES_PER_BANK
+                    if k >= 0 and k % TILES_PER_RUN == TILES_PER_RUN - 1:
+                        if k == TILES_PER_RUN - 1:
+                            y_ps = psum_acc.tile([P, TILES_PER_BANK, N_OUT], F32, tag="acc")
+                            sum_tiles.append(y_ps)
+                        for tile_in_bank in range(k - TILES_PER_RUN + 1, k + 1):
+                            multiply_row_tile(bank, tile_in_bank)
+                        if k == TILES_PER_BANK - 1:
+                            y_sb = ypool.tile([P, TILES_PER_BANK, N_OUT], F32)
+                            nc.scalar.copy(out=y_sb[:], in_=sum_tiles[bank][:])
+                            copy_tiles.append(y_sb)
+                if 0 <= step - STORE_LAG < UNITS:
+                    bank, within = order[step - STORE_LAG]
+                    if within == UNITS_PER_BANK - 1:
+                        leaky_relu_and_store(bank, copy_tiles[bank])

@@ -13,6 +13,7 @@ ACT = mybir.ActivationFunctionType
 
 P = 128
 PACK = 4
+PAIR = 2
 K_PASS = P * PACK
 N_NODES = 4096
 N_FEAT = 512
@@ -21,22 +22,24 @@ LEAKY_SLOPE = 0.01
 
 ROW_TILES = N_NODES // P
 PASSES = N_NODES // K_PASS
-HALF = N_NODES // 2
-PASSES_PER_UNIT = HALF // K_PASS
-UNITS = 2 * ROW_TILES
-GROUP_TILES = 8
-GROUPS = ROW_TILES // GROUP_TILES
-VECTOR_SUM_COLS = 2688
+CHUNK = 1024
+CHUNKS = N_NODES // CHUNK
+CHUNK_PASSES = CHUNK // K_PASS
+GROUP_TILES = CHUNK // P
+VECTOR_SUM_COLS = (2688, 2048, 1024, 512)
 TILES_PER_BANK = 4
-UNITS_PER_BANK = 2 * TILES_PER_BANK
-BANKS = ROW_TILES // TILES_PER_BANK
-EARLY_UNITS = TILES_PER_BANK
-EARLY_EVERY = 4
-PREFETCH = 4
-QUANT_LAG = 4
-MATMUL_LAG = QUANT_LAG + 1
 TILES_PER_RUN = 2
-STORE_LAG = MATMUL_LAG + 3
+
+ROW_AHEAD = 4
+Z_AHEAD = 2
+X_AHEAD = 6
+COPY_LAG = 1
+QUANT_LAG = 3
+MATMUL_LAG = 4
+YCOPY_LAG = 5
+STORE_LAG = 6
+D_LAG = 2
+FIRST_UNIT_STEP = GROUP_TILES + D_LAG
 
 FLOPS = 2 * N_NODES * N_FEAT * N_OUT + 2 * N_NODES * N_NODES * N_OUT
 
@@ -45,140 +48,87 @@ def tile_gcnlayer_pb_t_kernel(tc, A1, Hn, Wout, bout, out):
     nc = tc.nc
     with ExitStack() as ctx:
         keep = ctx.enter_context(tc.tile_pool(name="keep", bufs=1))
-        xpool = ctx.enter_context(tc.tile_pool(name="xpool", bufs=PREFETCH + 2))
-        psum_t = ctx.enter_context(tc.psum_pool(name="psum_t", bufs=6))
-        psum_acc = ctx.enter_context(tc.psum_pool(name="psum_acc", bufs=2))
-        dpool = ctx.enter_context(tc.tile_pool(name="dpool", bufs=2))
-        kept = ctx.enter_context(tc.tile_pool(name="kept", bufs=EARLY_UNITS))
+        rowpool = ctx.enter_context(tc.tile_pool(name="rowpool", bufs=ROW_AHEAD + 1))
+        junkpool = ctx.enter_context(tc.tile_pool(name="junkpool", bufs=2))
+        xpool = ctx.enter_context(tc.tile_pool(name="xpool", bufs=X_AHEAD + 2))
         hat_pool = ctx.enter_context(tc.tile_pool(name="hat_pool", bufs=3))
         grouped_pool = ctx.enter_context(tc.tile_pool(name="grouped_pool", bufs=QUANT_LAG + 2))
+        dpool = ctx.enter_context(tc.tile_pool(name="dpool", bufs=2))
+        ypool = ctx.enter_context(tc.tile_pool(name="ypool", bufs=2))
+        psum_t = ctx.enter_context(tc.psum_pool(name="psum_t", bufs=6))
+        psum_acc = ctx.enter_context(tc.psum_pool(name="psum_acc", bufs=2))
 
-        ident_bf = keep.tile([P, P], BF16)
-        make_identity(nc, ident_bf[:])
-        ident_f = keep.tile([P, P], F32)
-        make_identity(nc, ident_f[:])
+        ident = keep.tile([P, P], F32)
+        make_identity(nc, ident[:])
 
         one = keep.tile([P, 1], F32)
         nc.vector.memset(one[:], 1.0)
         warm = keep.tile([P, 1], F32)
-        nc.scalar.sqrt(warm[:], one[:])
+        nc.scalar.activation(out=warm[:], in_=one[:], func=ACT.Abs_reciprocal_sqrt)
 
         z_codes = keep.tile([P, PASSES, N_OUT], U32, align_bytes=64)
         z_scales = keep.tile([P, PASSES, N_OUT], U8, align_bytes=64)
-        with tc.tile_pool(name="zstage", bufs=2) as zstage, tc.tile_pool(name="zkeep", bufs=1) as zkeep:
-            w_raw = zkeep.tile([P, PACK, N_OUT], BF16)
-            for u in range(2):
-                nc.sync.dma_start(
-                    out=w_raw[:, 2 * u : 2 * u + 2, :],
-                    in_=Wout[256 * u : 256 * (u + 1), :].rearrange("(p e) o -> p e o", e=2),
-                )
-            bias_bc = zkeep.tile([P, N_OUT], BF16)
-            nc.sync.dma_start(out=bias_bc[:], in_=bout.partition_broadcast(P))
-            w_grouped = zkeep.tile([P, N_OUT, PACK], BF16, align_bytes=64)
-            nc.vector.tensor_copy(out=w_grouped[:], in_=w_raw[:].rearrange("p t o -> p o t"))
-            w_codes = zkeep.tile([P, N_OUT], U32, align_bytes=64)
-            w_scales = zkeep.tile([P, N_OUT], U8, align_bytes=64)
-            nc.vector.quantize_mx(
-                out=w_codes[:].bitcast(FP8X4),
-                scales=w_scales[:],
-                in_=w_grouped[:].rearrange("p o t -> p (o t)"),
-            )
-
-            z_grouped = zkeep.tile([P, PASSES, N_OUT, PACK], BF16, align_bytes=64)
-            for c in range(GROUPS):
-                hn = zstage.tile([P, GROUP_TILES * N_FEAT], BF16)
-                nc.sync.dma_start(
-                    out=hn[:].rearrange("m (n f) -> m n f", f=N_FEAT),
-                    in_=Hn[c * GROUP_TILES * P : (c + 1) * GROUP_TILES * P, :].rearrange(
-                        "(n m) f -> m n f", m=P
-                    ),
-                )
-                hn_words = hn[:].bitcast(F32)
-                h_grouped = zstage.tile([P, GROUP_TILES * K_PASS], BF16, align_bytes=64)
-                h_grouped_words = h_grouped[:].bitcast(F32).rearrange(
-                    "p (n m u) -> p n m u", m=P, u=2
-                )
-                for pair in range(GROUP_TILES // 2):
-                    h_ps = psum_t.tile([P, 2, 2, P], F32, tag="tp")
-                    for a in range(2):
-                        for u in range(2):
-                            first = (2 * pair + a) * (N_FEAT // 2) + u * P
-                            nc.tensor.transpose(
-                                h_ps[:, a, u, :], hn_words[:, first : first + P], ident_f[:]
-                            )
-                    nc.scalar.copy(
-                        out=h_grouped_words[:, 2 * pair : 2 * pair + 2, :, :],
-                        in_=h_ps[:].rearrange("p a u m -> p a m u"),
-                    )
-                h_codes = zstage.tile([P, GROUP_TILES, P], U32, align_bytes=64)
-                h_scales = zstage.tile([P, GROUP_TILES, P], U8, align_bytes=64)
-                nc.vector.quantize_mx(
-                    out=h_codes[:].rearrange("p n m -> p (n m)").bitcast(FP8X4),
-                    scales=h_scales[:].rearrange("p n m -> p (n m)"),
-                    in_=h_grouped[:],
-                )
-                for half in range(GROUP_TILES // PACK):
-                    g = c * (GROUP_TILES // PACK) + half
-                    z_ps = psum_acc.tile([P, PACK, N_OUT], F32, tag="acc")
-                    for t in range(PACK):
-                        n = half * PACK + t
-                        nc.tensor.matmul_mx(
-                            out=z_ps[:, t, :],
-                            lhsT=h_codes[:, n, :].bitcast(FP8X4),
-                            lhsT_scale=h_scales[:, n, :],
-                            rhs=w_codes[:].bitcast(FP8X4),
-                            rhs_scale=w_scales[:],
-                            start=True,
-                            stop=True,
-                        )
-                    nc.vector.tensor_tensor(
-                        out=z_grouped[:, g, :, :],
-                        in0=z_ps[:].rearrange("p t o -> p o t"),
-                        in1=bias_bc[:].unsqueeze(2).to_broadcast([P, N_OUT, PACK]),
-                        op=ALU.add,
-                    )
-            nc.vector.quantize_mx(
-                out=z_codes[:].rearrange("p g o -> p (g o)").bitcast(FP8X4),
-                scales=z_scales[:].rearrange("p g o -> p (g o)"),
-                in_=z_grouped[:].rearrange("p g o t -> p (g o t)"),
-            )
-
         d_rows = keep.tile([P, ROW_TILES], F32)
         d_cols = keep.tile([P, N_NODES], F32)
         sums_v = keep.tile([P, ROW_TILES], F32)
-        sums_s = keep.tile([P, ROW_TILES], F32)
+        sums_s0 = keep.tile([P, ROW_TILES], F32)
+        sums_s1 = keep.tile([P, ROW_TILES], F32)
+        sums_s = (sums_s0, sums_s1)
 
-        def begin_d(q):
+        row_tiles = []
+
+        def load_rows(r):
+            rows = rowpool.tile([P, N_NODES], BF16)
+            nc.sync.dma_start(out=rows[:], in_=A1[r * P : (r + 1) * P, :])
+            row_tiles.append(rows)
+
+        def sum_rows_vector(r):
+            cols = VECTOR_SUM_COLS[r // GROUP_TILES]
+            junk_v = junkpool.tile([P, VECTOR_SUM_COLS[0]], BF16)
+            nc.vector.tensor_scalar(
+                out=junk_v[:, :cols],
+                in0=row_tiles[r][:, :cols],
+                scalar1=1.0,
+                scalar2=None,
+                op0=ALU.mult,
+                op1=ALU.add,
+                accum_out=sums_v[:, r : r + 1],
+            )
+
+        def sum_rows_scalar(r, piece):
+            cols = VECTOR_SUM_COLS[r // GROUP_TILES]
+            width = (N_NODES - cols) // 2
+            first = cols + piece * width
+            junk_s = junkpool.tile([P, (N_NODES - VECTOR_SUM_COLS[-1]) // 2], BF16)
+            nc.scalar.activation(
+                out=junk_s[:, :width],
+                in_=row_tiles[r][:, first : first + width],
+                func=ACT.Copy,
+                accum_out=sums_s[piece][:, r : r + 1],
+            )
+
+        def d_of_rows(q):
             tiles = slice(q * GROUP_TILES, (q + 1) * GROUP_TILES)
             rowsum = dpool.tile([P, GROUP_TILES], F32)
-            nc.vector.tensor_tensor(
-                out=rowsum[:], in0=sums_v[:, tiles], in1=sums_s[:, tiles], op=ALU.add
-            )
-            root = dpool.tile([P, GROUP_TILES], F32)
-            nc.scalar.sqrt(root[:], rowsum[:])
-            return rowsum, root
-
-        def finish_d(q, rowsum, root):
-            tiles = slice(q * GROUP_TILES, (q + 1) * GROUP_TILES)
+            nc.gpsimd.tensor_tensor(out=rowsum[:], in0=sums_v[:, tiles], in1=sums_s0[:, tiles], op=ALU.add)
+            nc.gpsimd.tensor_tensor(out=rowsum[:], in0=rowsum[:], in1=sums_s1[:, tiles], op=ALU.add)
             guess = dpool.tile([P, GROUP_TILES], F32)
-            nc.vector.reciprocal(guess[:], root[:])
+            nc.scalar.activation(out=guess[:], in_=rowsum[:], func=ACT.Abs_reciprocal_sqrt)
             corr = dpool.tile([P, GROUP_TILES], F32)
-            nc.vector.tensor_tensor(out=corr[:], in0=guess[:], in1=guess[:], op=ALU.mult)
-            nc.vector.tensor_tensor(out=corr[:], in0=corr[:], in1=rowsum[:], op=ALU.mult)
-            nc.vector.tensor_scalar(
+            nc.gpsimd.tensor_tensor(out=corr[:], in0=guess[:], in1=guess[:], op=ALU.mult)
+            nc.gpsimd.tensor_tensor(out=corr[:], in0=corr[:], in1=rowsum[:], op=ALU.mult)
+            nc.gpsimd.tensor_scalar(
                 out=corr[:], in0=corr[:], scalar1=-0.5, scalar2=1.5, op0=ALU.mult, op1=ALU.add
             )
-            nc.vector.tensor_tensor(out=d_rows[:, tiles], in0=guess[:], in1=corr[:], op=ALU.mult)
-            repeated = dpool.tile([P, GROUP_TILES, P], F32)
-            nc.vector.tensor_copy(
-                out=repeated[:],
-                in_=d_rows[:, tiles].unsqueeze(2).to_broadcast([P, GROUP_TILES, P]),
-            )
+            nc.gpsimd.tensor_tensor(out=d_rows[:, tiles], in0=guess[:], in1=corr[:], op=ALU.mult)
+
+        def d_along_columns(q):
             for bank in range(GROUP_TILES // TILES_PER_BANK):
                 d_ps = psum_t.tile([P, TILES_PER_BANK, P], F32, tag="tp")
                 for a in range(TILES_PER_BANK):
+                    r = q * GROUP_TILES + bank * TILES_PER_BANK + a
                     nc.tensor.transpose(
-                        d_ps[:, a, :], repeated[:, bank * TILES_PER_BANK + a, :], ident_f[:]
+                        d_ps[:, a, :], d_rows[:, r : r + 1].to_broadcast([P, P]), ident[:]
                     )
                 first = (q * GROUP_TILES + bank * TILES_PER_BANK) * P
                 nc.scalar.copy(
@@ -186,122 +136,103 @@ def tile_gcnlayer_pb_t_kernel(tc, A1, Hn, Wout, bout, out):
                     in_=d_ps[:].rearrange("p a n -> p (a n)"),
                 )
 
-        def half_bank(bank, h):
-            return [(bank, h * TILES_PER_BANK + k) for k in range(TILES_PER_BANK)]
+        by_group = []
+        for q in range(CHUNKS):
+            fresh = [(r, q) for r in range(q * GROUP_TILES)]
+            for r in range(q * GROUP_TILES, (q + 1) * GROUP_TILES):
+                fresh.extend([(r, c) for c in range(q + 1)])
+            by_group.append(fresh)
+        order = [unit for fresh in by_group for unit in fresh]
 
-        order = half_bank(0, 0)
-        for bank in range(BANKS):
-            if bank + 1 < BANKS:
-                order.extend(half_bank(bank + 1, 0))
-            order.extend(half_bank(bank, 1))
+        def units_at_step(step):
+            q, s = divmod(step - FIRST_UNIT_STEP, GROUP_TILES)
+            if q < 0 or q >= CHUNKS - 1:
+                return 0
+            return len(by_group[q]) // GROUP_TILES
 
-        def row_tile_and_half(unit):
-            bank, within = unit
-            h, k = divmod(within, TILES_PER_BANK)
-            return bank * TILES_PER_BANK + k, h
+        x_tiles = []
+        grouped_tiles = []
+        transposed = []
+        code_tiles = {}
+        sum_tiles = []
+        copy_tiles = []
 
-        kept_rows = []
+        def fetch_unit(k):
+            r, c = order[k]
+            x = xpool.tile([P, CHUNK], BF16)
+            nc.sync.dma_start(out=x[:], in_=A1[r * P : (r + 1) * P, c * CHUNK : (c + 1) * CHUNK])
+            x_tiles.append(x)
 
-        def fetch_unit(unit):
-            r, h = row_tile_and_half(unit)
-            if r < len(kept_rows):
-                return kept_rows[r][:, h * HALF : (h + 1) * HALF]
-            x = xpool.tile([P, HALF], BF16)
-            nc.sync.dma_start(out=x[:], in_=A1[r * P : (r + 1) * P, h * HALF : (h + 1) * HALF])
-            return x[:]
-
-        def scale_and_transpose(unit, x):
-            r, h = row_tile_and_half(unit)
-            a_hat = hat_pool.tile([P, HALF], BF16)
+        def scale_and_transpose(k):
+            r, c = order[k]
+            a_hat = hat_pool.tile([P, CHUNK], BF16)
             nc.vector.scalar_tensor_tensor(
                 out=a_hat[:],
-                in0=x,
+                in0=x_tiles[k][:],
                 scalar=d_rows[:, r : r + 1],
-                in1=d_cols[:, h * HALF : (h + 1) * HALF],
+                in1=d_cols[:, c * CHUNK : (c + 1) * CHUNK],
                 op0=ALU.mult,
                 op1=ALU.mult,
             )
-            grouped = grouped_pool.tile([P, PASSES_PER_UNIT, P, PACK], BF16, align_bytes=64)
-            for g in range(PASSES_PER_UNIT):
-                a_ps = psum_t.tile([P, PACK, P], BF16, tag="tp")
-                for t in range(PACK):
-                    first = (g * PACK + t) * P
-                    nc.tensor.transpose(a_ps[:, t, :], a_hat[:, first : first + P], ident_bf[:])
-                nc.scalar.copy(out=grouped[:, g, :, :], in_=a_ps[:].rearrange("p t i -> p i t"))
-            return grouped
+            words = a_hat[:].bitcast(F32)
+            a_ps = psum_t.tile([P, CHUNK_PASSES, PAIR, P], F32, tag="tp")
+            for g in range(CHUNK_PASSES):
+                for u in range(PAIR):
+                    first = (g * PAIR + u) * P
+                    nc.tensor.transpose(a_ps[:, g, u, :], words[:, first : first + P], ident[:])
+            transposed.append(a_ps)
 
-        grouped_tiles = []
-
-        with tc.tile_pool(name="rowpool", bufs=5) as rowpool, tc.tile_pool(name="sumpool", bufs=1) as sumpool:
-            junk_v = sumpool.tile([P, VECTOR_SUM_COLS], BF16)
-            junk_s = sumpool.tile([P, N_NODES - VECTOR_SUM_COLS], BF16)
-            for q in range(GROUPS):
-                for r in range(q * GROUP_TILES, (q + 1) * GROUP_TILES):
-                    if r < EARLY_UNITS:
-                        rows = kept.tile([P, N_NODES], BF16)
-                        kept_rows.append(rows)
-                    else:
-                        rows = rowpool.tile([P, N_NODES], BF16)
-                    nc.sync.dma_start(out=rows[:], in_=A1[r * P : (r + 1) * P, :])
-                    nc.vector.tensor_scalar(
-                        out=junk_v[:],
-                        in0=rows[:, :VECTOR_SUM_COLS],
-                        scalar1=1.0,
-                        scalar2=None,
-                        op0=ALU.mult,
-                        op1=ALU.add,
-                        accum_out=sums_v[:, r : r + 1],
-                    )
-                    nc.scalar.activation(
-                        out=junk_s[:],
-                        in_=rows[:, VECTOR_SUM_COLS:],
-                        func=ACT.Copy,
-                        accum_out=sums_s[:, r : r + 1],
-                    )
-                    if r >= ROW_TILES // 2 and r % EARLY_EVERY == 0:
-                        unit = order[len(grouped_tiles)]
-                        grouped_tiles.append(scale_and_transpose(unit, fetch_unit(unit)))
-                rowsum, root = begin_d(q)
-                if q < GROUPS - 1:
-                    finish_d(q, rowsum, root)
-
-        codes_pool = ctx.enter_context(tc.tile_pool(name="codes_pool", bufs=3))
-        ypool = ctx.enter_context(tc.tile_pool(name="ypool", bufs=2))
-        out_tiles = out.rearrange("(r p) o -> p r o", p=P)
-        bank_shape = [P, UNITS_PER_BANK, PASSES_PER_UNIT, P]
-
-        def quantise(unit, grouped):
-            bank, within = unit
-            a_codes, a_scales = code_tiles[bank]
-            nc.vector.quantize_mx(
-                out=a_codes[:, within, :, :].rearrange("p g i -> p (g i)").bitcast(FP8X4),
-                scales=a_scales[:, within, :, :].rearrange("p g i -> p (g i)"),
-                in_=grouped[:].rearrange("p g i t -> p (g i t)"),
+        def group_words(k):
+            grouped = grouped_pool.tile([P, CHUNK_PASSES, P, PACK], BF16, align_bytes=64)
+            grouped_words = grouped[:].rearrange("p g i t -> p (g i t)").bitcast(F32)
+            nc.scalar.copy(
+                out=grouped_words.rearrange("p (g i u) -> p g i u", i=P, u=PAIR),
+                in_=transposed[k][:].rearrange("p g u i -> p g i u"),
             )
+            grouped_tiles.append(grouped)
 
-        def multiply_row_tile(bank, k):
-            a_codes, a_scales = code_tiles[bank]
+        def quantise(k):
+            a_codes = codes_pool.tile([P, CHUNK_PASSES, P], U32, align_bytes=64)
+            a_scales = codes_pool.tile([P, CHUNK_PASSES, P], U8, align_bytes=64)
+            nc.vector.quantize_mx(
+                out=a_codes[:].rearrange("p g i -> p (g i)").bitcast(FP8X4),
+                scales=a_scales[:].rearrange("p g i -> p (g i)"),
+                in_=grouped_tiles[k][:].rearrange("p g i t -> p (g i t)"),
+            )
+            code_tiles[order[k]] = (a_codes, a_scales)
+
+        def multiply_row_tile(r):
+            bank, slot = divmod(r, TILES_PER_BANK)
+            if slot == 0:
+                y_ps = psum_acc.tile([P, TILES_PER_BANK, N_OUT], F32, tag="acc")
+                sum_tiles.append(y_ps)
             for z_pass in range(PASSES):
-                h, g = divmod(z_pass, PASSES_PER_UNIT)
-                within = h * TILES_PER_BANK + k
+                c, g = divmod(z_pass, CHUNK_PASSES)
+                a_codes, a_scales = code_tiles[(r, c)]
                 nc.tensor.matmul_mx(
-                    out=sum_tiles[bank][:, k, :],
-                    lhsT=a_codes[:, within, g, :].bitcast(FP8X4),
-                    lhsT_scale=a_scales[:, within, g, :],
+                    out=sum_tiles[bank][:, slot, :],
+                    lhsT=a_codes[:, g, :].bitcast(FP8X4),
+                    lhsT_scale=a_scales[:, g, :],
                     rhs=z_codes[:, z_pass, :].bitcast(FP8X4),
                     rhs_scale=z_scales[:, z_pass, :],
                     start=(z_pass == 0),
                     stop=(z_pass == PASSES - 1),
                 )
 
-        def leaky_relu_and_store(bank, y_sb):
-            y_ps = sum_tiles[bank]
+        out_tiles = out.rearrange("(r p) o -> p r o", p=P)
+
+        def copy_sums(bank):
+            y_sb = ypool.tile([P, TILES_PER_BANK * N_OUT], F32)
+            nc.scalar.copy(out=y_sb[:], in_=sum_tiles[bank][:].rearrange("p r o -> p (r o)"))
+            copy_tiles.append(y_sb)
+
+        def leaky_relu_and_store(bank):
             result = ypool.tile([P, TILES_PER_BANK, N_OUT], F32)
             nc.vector.scalar_tensor_tensor(
                 out=result[:].rearrange("p r o -> p (r o)"),
-                in0=y_ps[:].rearrange("p r o -> p (r o)"),
+                in0=sum_tiles[bank][:].rearrange("p r o -> p (r o)"),
                 scalar=LEAKY_SLOPE,
-                in1=y_sb[:].rearrange("p r o -> p (r o)"),
+                in1=copy_tiles[bank][:],
                 op0=ALU.mult,
                 op1=ALU.max,
             )
@@ -310,41 +241,167 @@ def tile_gcnlayer_pb_t_kernel(tc, A1, Hn, Wout, bout, out):
                 out=out_tiles[:, first_tile : first_tile + TILES_PER_BANK, :], in_=result[:]
             )
 
-        code_tiles = []
-        sum_tiles = []
-        copy_tiles = []
-        x_views = [None] * EARLY_UNITS
-        for step in range(EARLY_UNITS, EARLY_UNITS + PREFETCH):
-            x_views.append(fetch_unit(order[step]))
+        def last_unit_of(k):
+            if 0 <= k < len(order) and order[k][1] == CHUNKS - 1:
+                return order[k][0]
+            return -1
+
+        def work_on_unit(k):
+            if k + X_AHEAD < len(order):
+                fetch_unit(k + X_AHEAD)
+            if k < len(order):
+                scale_and_transpose(k)
+            if 0 <= k - COPY_LAG < len(order):
+                group_words(k - COPY_LAG)
+            if 0 <= k - QUANT_LAG < len(order):
+                quantise(k - QUANT_LAG)
+            r = last_unit_of(k - MATMUL_LAG)
+            if r % TILES_PER_RUN == TILES_PER_RUN - 1 and r >= 0:
+                for tile in range(r - TILES_PER_RUN + 1, r + 1):
+                    multiply_row_tile(tile)
+            r = last_unit_of(k - YCOPY_LAG)
+            if r % TILES_PER_BANK == TILES_PER_BANK - 1 and r >= 0:
+                copy_sums(r // TILES_PER_BANK)
+            r = last_unit_of(k - STORE_LAG)
+            if r % TILES_PER_BANK == TILES_PER_BANK - 1 and r >= 0:
+                leaky_relu_and_store(r // TILES_PER_BANK)
+
+        hn_tiles = []
+        h_grouped_tiles = []
+        z_sums = []
+
         with tc.manual_schedule():
-            for step in range(EARLY_UNITS, UNITS + STORE_LAG):
-                if step + PREFETCH < UNITS:
-                    x_views.append(fetch_unit(order[step + PREFETCH]))
-                if step < UNITS:
-                    grouped_tiles.append(scale_and_transpose(order[step], x_views[step]))
-                if step == EARLY_UNITS:
-                    finish_d(GROUPS - 1, rowsum, root)
-                if 0 <= step - QUANT_LAG < UNITS:
-                    unit = order[step - QUANT_LAG]
-                    if unit[1] == 0:
-                        a_codes = codes_pool.tile(bank_shape, U32, align_bytes=64)
-                        a_scales = codes_pool.tile(bank_shape, U8, align_bytes=64)
-                        code_tiles.append((a_codes, a_scales))
-                    quantise(unit, grouped_tiles[step - QUANT_LAG])
-                if 0 <= step - MATMUL_LAG < UNITS:
-                    bank, within = order[step - MATMUL_LAG]
-                    k = within - TILES_PER_BANK
-                    if k >= 0 and k % TILES_PER_RUN == TILES_PER_RUN - 1:
-                        if k == TILES_PER_RUN - 1:
-                            y_ps = psum_acc.tile([P, TILES_PER_BANK, N_OUT], F32, tag="acc")
-                            sum_tiles.append(y_ps)
-                        for tile_in_bank in range(k - TILES_PER_RUN + 1, k + 1):
-                            multiply_row_tile(bank, tile_in_bank)
-                        if k == TILES_PER_BANK - 1:
-                            y_sb = ypool.tile([P, TILES_PER_BANK, N_OUT], F32)
-                            nc.scalar.copy(out=y_sb[:], in_=sum_tiles[bank][:])
-                            copy_tiles.append(y_sb)
-                if 0 <= step - STORE_LAG < UNITS:
-                    bank, within = order[step - STORE_LAG]
-                    if within == UNITS_PER_BANK - 1:
-                        leaky_relu_and_store(bank, copy_tiles[bank])
+            with tc.tile_pool(name="zstage", bufs=2) as zstage, tc.tile_pool(name="zkeep", bufs=1) as zkeep, tc.tile_pool(name="hpool", bufs=Z_AHEAD + 1) as hpool:
+
+                def load_h(g):
+                    hn = hpool.tile([P, PACK, N_FEAT], BF16)
+                    nc.sync.dma_start(
+                        out=hn[:].rearrange("m (u e) f -> m u e f", e=PAIR),
+                        in_=Hn[g * K_PASS : (g + 1) * K_PASS, :].rearrange(
+                            "(u m e) f -> m u e f", m=P, e=PAIR
+                        ),
+                    )
+                    hn_tiles.append(hn)
+
+                def transpose_h(g):
+                    words = hn_tiles[g][:].rearrange("m t f -> m (t f)").bitcast(F32)
+                    h_grouped = zstage.tile([P, PACK * P * PACK], BF16, align_bytes=64)
+                    h_words = h_grouped[:].bitcast(F32).rearrange("p (t m u) -> p t m u", m=P, u=PAIR)
+                    for half in range(2):
+                        h_ps = psum_t.tile([P, PAIR, PAIR, P], F32, tag="tp")
+                        for a in range(PAIR):
+                            for u in range(PAIR):
+                                first = ((half * PAIR + a) * PAIR + u) * P
+                                nc.tensor.transpose(h_ps[:, a, u, :], words[:, first : first + P], ident[:])
+                        nc.scalar.copy(
+                            out=h_words[:, half * PAIR : (half + 1) * PAIR, :, :],
+                            in_=h_ps[:].rearrange("p a u m -> p a m u"),
+                        )
+                    h_grouped_tiles.append(h_grouped)
+
+                def multiply_h(g):
+                    h_codes = zstage.tile([P, PACK, P], U32, align_bytes=64)
+                    h_scales = zstage.tile([P, PACK, P], U8, align_bytes=64)
+                    nc.vector.quantize_mx(
+                        out=h_codes[:].rearrange("p t m -> p (t m)").bitcast(FP8X4),
+                        scales=h_scales[:].rearrange("p t m -> p (t m)"),
+                        in_=h_grouped_tiles[g][:],
+                    )
+                    z_ps = psum_acc.tile([P, PACK, N_OUT], F32, tag="acc")
+                    for t in range(PACK):
+                        nc.tensor.matmul_mx(
+                            out=z_ps[:, t, :],
+                            lhsT=h_codes[:, t, :].bitcast(FP8X4),
+                            lhsT_scale=h_scales[:, t, :],
+                            rhs=w_codes[:].bitcast(FP8X4),
+                            rhs_scale=w_scales[:],
+                            start=True,
+                            stop=True,
+                        )
+                    z_sums.append(z_ps)
+
+                def add_bias(g):
+                    nc.vector.tensor_tensor(
+                        out=z_grouped[:, g, :, :],
+                        in0=z_sums[g][:].rearrange("p t o -> p o t"),
+                        in1=bias_bc[:].unsqueeze(2).to_broadcast([P, N_OUT, PACK]),
+                        op=ALU.add,
+                    )
+
+                load_rows(0)
+                w_raw = zkeep.tile([P, PACK, N_OUT], BF16)
+                for u in range(PAIR):
+                    nc.sync.dma_start(
+                        out=w_raw[:, PAIR * u : PAIR * (u + 1), :],
+                        in_=Wout[256 * u : 256 * (u + 1), :].rearrange("(p e) o -> p e o", e=PAIR),
+                    )
+                load_h(0)
+                load_rows(1)
+                load_h(1)
+                bias_bc = zkeep.tile([P, N_OUT], BF16)
+                nc.sync.dma_start(out=bias_bc[:], in_=bout.partition_broadcast(P))
+                load_rows(2)
+                load_rows(3)
+
+                sum_rows_vector(0)
+                w_grouped = zkeep.tile([P, N_OUT, PACK], BF16, align_bytes=64)
+                nc.vector.tensor_copy(out=w_grouped[:], in_=w_raw[:].rearrange("p t o -> p o t"))
+                w_codes = zkeep.tile([P, N_OUT], U32, align_bytes=64)
+                w_scales = zkeep.tile([P, N_OUT], U8, align_bytes=64)
+                z_grouped = zkeep.tile([P, PASSES, N_OUT, PACK], BF16, align_bytes=64)
+
+                for step in range(FIRST_UNIT_STEP):
+                    load_rows(step + ROW_AHEAD)
+                    if step + Z_AHEAD < PASSES:
+                        load_h(step + Z_AHEAD)
+                    if step == FIRST_UNIT_STEP - 1:
+                        for k in range(X_AHEAD):
+                            fetch_unit(k)
+                    if step == GROUP_TILES:
+                        d_of_rows(0)
+                    if step == GROUP_TILES + 1:
+                        d_along_columns(0)
+                    if step > 0:
+                        sum_rows_vector(step)
+                    if step < PASSES:
+                        transpose_h(step)
+                    sum_rows_scalar(step, 0)
+                    sum_rows_scalar(step, 1)
+                    if step == 1:
+                        nc.vector.quantize_mx(
+                            out=w_codes[:].bitcast(FP8X4),
+                            scales=w_scales[:],
+                            in_=w_grouped[:].rearrange("p o t -> p (o t)"),
+                        )
+                    if 0 <= step - 1 < PASSES:
+                        multiply_h(step - 1)
+                    if 0 <= step - 2 < PASSES:
+                        add_bias(step - 2)
+                nc.vector.quantize_mx(
+                    out=z_codes[:].rearrange("p g o -> p (g o)").bitcast(FP8X4),
+                    scales=z_scales[:].rearrange("p g o -> p (g o)"),
+                    in_=z_grouped[:].rearrange("p g o t -> p (g o t)"),
+                )
+
+            codes_pool = ctx.enter_context(tc.tile_pool(name="codes_pool", bufs=84))
+            k = 0
+            for step in range(FIRST_UNIT_STEP, ROW_TILES + D_LAG):
+                if step + ROW_AHEAD < ROW_TILES:
+                    load_rows(step + ROW_AHEAD)
+                q, s = divmod(step, GROUP_TILES)
+                if s == 0:
+                    d_of_rows(q - 1)
+                if s == 1:
+                    d_along_columns(q - 1)
+                if step < ROW_TILES:
+                    sum_rows_vector(step)
+                    sum_rows_scalar(step, 0)
+                count = units_at_step(step)
+                for i in range(count):
+                    work_on_unit(k)
+                    k += 1
+                    if i == count // 2 and step < ROW_TILES:
+                        sum_rows_scalar(step, 1)
+            while k < len(order) + STORE_LAG:
+                work_on_unit(k)
+                k += 1

@@ -22,24 +22,30 @@ LEAKY_SLOPE = 0.01
 
 ROW_TILES = N_NODES // P
 PASSES = N_NODES // K_PASS
-CHUNK = 1024
-CHUNKS = N_NODES // CHUNK
-CHUNK_PASSES = CHUNK // K_PASS
-GROUP_TILES = CHUNK // P
-VECTOR_SUM_COLS = (2688, 2048, 1024, 512)
+GROUP_TILES = (8, 8, 8, 8)
+VECTOR_SUM_COLS = (2688, 2304, 1280, 1024)
+GROUPS = len(GROUP_TILES)
+FIRST_TILE = [sum(GROUP_TILES[:q]) for q in range(GROUPS + 1)]
+GROUP_OF = [q for q in range(GROUPS) for r in range(GROUP_TILES[q])]
 TILES_PER_BANK = 4
 TILES_PER_RUN = 2
 
 ROW_AHEAD = 4
 Z_AHEAD = 2
-X_AHEAD = 6
+X_AHEAD = 7
 COPY_LAG = 1
-QUANT_LAG = 3
-MATMUL_LAG = 4
-YCOPY_LAG = 5
-STORE_LAG = 6
+QUANT_LAG = 4
+MATMUL_LAG = 5
+YCOPY_LAG = 6
+STORE_LAG = 9
+OFFLOAD_LEAD = 3
 D_LAG = 2
-FIRST_UNIT_STEP = GROUP_TILES + D_LAG
+Z_FIRST = 0
+Z_LAST = Z_FIRST + PASSES + 3
+UNIT_CHUNKS = 1
+CODES_BUFS = 84
+OFFLOAD_EVERY = 4
+BANK_PASSES = 2
 
 FLOPS = 2 * N_NODES * N_FEAT * N_OUT + 2 * N_NODES * N_NODES * N_OUT
 
@@ -49,12 +55,11 @@ def tile_gcnlayer_pb_t_kernel(tc, A1, Hn, Wout, bout, out):
     with ExitStack() as ctx:
         keep = ctx.enter_context(tc.tile_pool(name="keep", bufs=1))
         rowpool = ctx.enter_context(tc.tile_pool(name="rowpool", bufs=ROW_AHEAD + 1))
-        junkpool = ctx.enter_context(tc.tile_pool(name="junkpool", bufs=2))
         xpool = ctx.enter_context(tc.tile_pool(name="xpool", bufs=X_AHEAD + 2))
         hat_pool = ctx.enter_context(tc.tile_pool(name="hat_pool", bufs=3))
         grouped_pool = ctx.enter_context(tc.tile_pool(name="grouped_pool", bufs=QUANT_LAG + 2))
         dpool = ctx.enter_context(tc.tile_pool(name="dpool", bufs=2))
-        ypool = ctx.enter_context(tc.tile_pool(name="ypool", bufs=2))
+        codes_pool = ctx.enter_context(tc.tile_pool(name="codes_pool", bufs=CODES_BUFS))
         psum_t = ctx.enter_context(tc.psum_pool(name="psum_t", bufs=6))
         psum_acc = ctx.enter_context(tc.psum_pool(name="psum_acc", bufs=2))
 
@@ -69,11 +74,10 @@ def tile_gcnlayer_pb_t_kernel(tc, A1, Hn, Wout, bout, out):
         z_codes = keep.tile([P, PASSES, N_OUT], U32, align_bytes=64)
         z_scales = keep.tile([P, PASSES, N_OUT], U8, align_bytes=64)
         d_rows = keep.tile([P, ROW_TILES], F32)
+        d_words = keep.tile([P, ROW_TILES], F32)
         d_cols = keep.tile([P, N_NODES], F32)
         sums_v = keep.tile([P, ROW_TILES], F32)
-        sums_s0 = keep.tile([P, ROW_TILES], F32)
-        sums_s1 = keep.tile([P, ROW_TILES], F32)
-        sums_s = (sums_s0, sums_s1)
+        sums_s = keep.tile([P, ROW_TILES], F32)
 
         row_tiles = []
 
@@ -83,11 +87,10 @@ def tile_gcnlayer_pb_t_kernel(tc, A1, Hn, Wout, bout, out):
             row_tiles.append(rows)
 
         def sum_rows_vector(r):
-            cols = VECTOR_SUM_COLS[r // GROUP_TILES]
-            junk_v = junkpool.tile([P, VECTOR_SUM_COLS[0]], BF16)
+            part = row_tiles[r][:, : VECTOR_SUM_COLS[GROUP_OF[r]]]
             nc.vector.tensor_scalar(
-                out=junk_v[:, :cols],
-                in0=row_tiles[r][:, :cols],
+                out=part,
+                in0=part,
                 scalar1=1.0,
                 scalar2=None,
                 op0=ALU.mult,
@@ -95,111 +98,194 @@ def tile_gcnlayer_pb_t_kernel(tc, A1, Hn, Wout, bout, out):
                 accum_out=sums_v[:, r : r + 1],
             )
 
-        def sum_rows_scalar(r, piece):
-            cols = VECTOR_SUM_COLS[r // GROUP_TILES]
-            width = (N_NODES - cols) // 2
-            first = cols + piece * width
-            junk_s = junkpool.tile([P, (N_NODES - VECTOR_SUM_COLS[-1]) // 2], BF16)
-            nc.scalar.activation(
-                out=junk_s[:, :width],
-                in_=row_tiles[r][:, first : first + width],
-                func=ACT.Copy,
-                accum_out=sums_s[piece][:, r : r + 1],
+        def sum_rows_scalar(r):
+            part = row_tiles[r][:, VECTOR_SUM_COLS[GROUP_OF[r]] :]
+            nc.scalar.activation(out=part, in_=part, func=ACT.Copy, accum_out=sums_s[:, r : r + 1])
+
+        d_parts = {}
+
+        def add_row_sums(q):
+            tiles = slice(FIRST_TILE[q], FIRST_TILE[q + 1])
+            rowsum = dpool.tile([P, GROUP_TILES[q]], F32)
+            nc.vector.tensor_tensor(out=rowsum[:], in0=sums_v[:, tiles], in1=sums_s[:, tiles], op=ALU.add)
+            guess = dpool.tile([P, GROUP_TILES[q]], F32)
+            nc.scalar.activation(out=guess[:], in_=rowsum[:], func=ACT.Abs_reciprocal_sqrt)
+            d_parts[q] = (rowsum, guess)
+
+        def square_guess(q):
+            rowsum, guess = d_parts[q]
+            square = dpool.tile([P, GROUP_TILES[q]], F32)
+            nc.vector.tensor_tensor(out=square[:], in0=guess[:], in1=guess[:], op=ALU.mult)
+            d_parts[q] = (rowsum, guess, square)
+
+        def half_product(q):
+            rowsum, guess, square = d_parts[q]
+            product = dpool.tile([P, GROUP_TILES[q]], F32)
+            nc.vector.scalar_tensor_tensor(
+                out=product[:], in0=square[:], scalar=-0.5, in1=rowsum[:], op0=ALU.mult, op1=ALU.mult
             )
+            d_parts[q] = (guess, product)
 
         def d_of_rows(q):
-            tiles = slice(q * GROUP_TILES, (q + 1) * GROUP_TILES)
-            rowsum = dpool.tile([P, GROUP_TILES], F32)
-            nc.gpsimd.tensor_tensor(out=rowsum[:], in0=sums_v[:, tiles], in1=sums_s0[:, tiles], op=ALU.add)
-            nc.gpsimd.tensor_tensor(out=rowsum[:], in0=rowsum[:], in1=sums_s1[:, tiles], op=ALU.add)
-            guess = dpool.tile([P, GROUP_TILES], F32)
-            nc.scalar.activation(out=guess[:], in_=rowsum[:], func=ACT.Abs_reciprocal_sqrt)
-            corr = dpool.tile([P, GROUP_TILES], F32)
-            nc.gpsimd.tensor_tensor(out=corr[:], in0=guess[:], in1=guess[:], op=ALU.mult)
-            nc.gpsimd.tensor_tensor(out=corr[:], in0=corr[:], in1=rowsum[:], op=ALU.mult)
-            nc.gpsimd.tensor_scalar(
-                out=corr[:], in0=corr[:], scalar1=-0.5, scalar2=1.5, op0=ALU.mult, op1=ALU.add
+            guess, product = d_parts[q]
+            tiles = slice(FIRST_TILE[q], FIRST_TILE[q + 1])
+            nc.vector.scalar_tensor_tensor(
+                out=d_rows[:, tiles], in0=product[:], scalar=1.5, in1=guess[:], op0=ALU.add, op1=ALU.mult
             )
-            nc.gpsimd.tensor_tensor(out=d_rows[:, tiles], in0=guess[:], in1=corr[:], op=ALU.mult)
 
         def d_along_columns(q):
-            for bank in range(GROUP_TILES // TILES_PER_BANK):
+            for first in range(FIRST_TILE[q], FIRST_TILE[q + 1], TILES_PER_BANK):
                 d_ps = psum_t.tile([P, TILES_PER_BANK, P], F32, tag="tp")
                 for a in range(TILES_PER_BANK):
-                    r = q * GROUP_TILES + bank * TILES_PER_BANK + a
+                    r = first + a
                     nc.tensor.transpose(
                         d_ps[:, a, :], d_rows[:, r : r + 1].to_broadcast([P, P]), ident[:]
                     )
-                first = (q * GROUP_TILES + bank * TILES_PER_BANK) * P
                 nc.scalar.copy(
-                    out=d_cols[:, first : first + TILES_PER_BANK * P],
+                    out=d_cols[:, first * P : (first + TILES_PER_BANK) * P],
                     in_=d_ps[:].rearrange("p a n -> p (a n)"),
                 )
 
         by_group = []
-        for q in range(CHUNKS):
-            fresh = [(r, q) for r in range(q * GROUP_TILES)]
-            for r in range(q * GROUP_TILES, (q + 1) * GROUP_TILES):
-                fresh.extend([(r, c) for c in range(q + 1)])
+        for q in range(GROUPS):
+            fresh = [(r, q, q + 1) for r in range(FIRST_TILE[q])]
+            for r in range(FIRST_TILE[q], FIRST_TILE[q + 1]):
+                fresh.extend([(r, c, min(c + UNIT_CHUNKS, q + 1)) for c in range(0, q + 1, UNIT_CHUNKS)])
             by_group.append(fresh)
         order = [unit for fresh in by_group for unit in fresh]
 
         def units_at_step(step):
-            q, s = divmod(step - FIRST_UNIT_STEP, GROUP_TILES)
-            if q < 0 or q >= CHUNKS - 1:
-                return 0
-            return len(by_group[q]) // GROUP_TILES
+            for q in range(GROUPS - 1):
+                s = step - FIRST_TILE[q + 1] - D_LAG
+                n = GROUP_TILES[q + 1]
+                if 0 <= s < n:
+                    return len(by_group[q]) * (s + 1) // n - len(by_group[q]) * s // n
+            return 0
+
+        def columns_of(k):
+            r, c, end = order[k]
+            return FIRST_TILE[c] * P, FIRST_TILE[end] * P
 
         x_tiles = []
-        grouped_tiles = []
-        transposed = []
+        grouped_tiles = {}
+        transposed = {}
         code_tiles = {}
         sum_tiles = []
         copy_tiles = []
 
         def fetch_unit(k):
-            r, c = order[k]
-            x = xpool.tile([P, CHUNK], BF16)
-            nc.sync.dma_start(out=x[:], in_=A1[r * P : (r + 1) * P, c * CHUNK : (c + 1) * CHUNK])
+            r = order[k][0]
+            first, last = columns_of(k)
+            x = xpool.tile([P, last - first], BF16)
+            nc.sync.dma_start(out=x[:], in_=A1[r * P : (r + 1) * P, first:last])
             x_tiles.append(x)
 
+        def by_scalar(k):
+            first_late = len(order) - len(by_group[-1])
+            return first_late + OFFLOAD_LEAD <= k < len(order) - OFFLOAD_LEAD and (k - first_late) % OFFLOAD_EVERY == OFFLOAD_EVERY - 1
+
+        scaled_rows = {}
+        scaled_banks = {}
+        scaled_columns = {}
+
+        def scale_rows(k):
+            r = order[k][0]
+            first, last = columns_of(k)
+            half_hat = offload_pool.tile([P, last - first], F32)
+            nc.scalar.activation(out=half_hat[:], in_=x_tiles[k][:], func=ACT.Copy, scale=d_rows[:, r : r + 1])
+            scaled_rows[k] = half_hat
+
+        def transpose_half_hat(k):
+            first, last = columns_of(k)
+            banks = []
+            for g in range((last - first) // K_PASS):
+                t_ps = psum_t.tile([P, PACK, P], F32, tag="tp")
+                for t in range(PACK):
+                    u, e = divmod(t, PAIR)
+                    at = (g * PAIR + u) * PAIR * P + e
+                    nc.tensor.transpose(t_ps[:, t, :], scaled_rows[k][:, at : at + PAIR * P - 1 : PAIR], ident[:])
+                banks.append(t_ps)
+            scaled_banks[k] = banks
+
+        def scale_columns(k, g):
+            first, last = columns_of(k)
+            if g == 0:
+                hat_columns = offload_pool.tile([P, (last - first) // K_PASS, PACK, P], BF16)
+                scaled_columns[k] = hat_columns
+            for t in range(PACK):
+                at = first // P + g * PACK + t
+                nc.scalar.activation(
+                    out=scaled_columns[k][:, g, t, :],
+                    in_=scaled_banks[k][g][:, t, :],
+                    func=ACT.Copy,
+                    scale=d_words[:, at : at + 1],
+                )
+
+        def interleave(k):
+            first, last = columns_of(k)
+            grouped = grouped_pool.tile([P, (last - first) // K_PASS, P, PACK], BF16, align_bytes=64)
+            nc.scalar.copy(out=grouped[:], in_=scaled_columns[k][:].rearrange("p g t i -> p g i t"))
+            grouped_tiles[k] = grouped
+
+        def d_along_words(g):
+            d_ps = psum_t.tile([P, PACK, P], F32, tag="tp")
+            for t in range(PACK):
+                u, e = divmod(t, PAIR)
+                at = (g * PAIR + u) * PAIR * P + e
+                nc.tensor.transpose(d_ps[:, t, :], d_cols[:, at : at + PAIR * P - 1 : PAIR], ident[:])
+            nc.scalar.copy(out=d_words[:, g * PACK : (g + 1) * PACK], in_=d_ps[:, :, 0])
+
         def scale_and_transpose(k):
-            r, c = order[k]
-            a_hat = hat_pool.tile([P, CHUNK], BF16)
+            r = order[k][0]
+            first, last = columns_of(k)
+            a_hat = hat_pool.tile([P, last - first], BF16)
             nc.vector.scalar_tensor_tensor(
                 out=a_hat[:],
                 in0=x_tiles[k][:],
                 scalar=d_rows[:, r : r + 1],
-                in1=d_cols[:, c * CHUNK : (c + 1) * CHUNK],
+                in1=d_cols[:, first:last],
                 op0=ALU.mult,
                 op1=ALU.mult,
             )
             words = a_hat[:].bitcast(F32)
-            a_ps = psum_t.tile([P, CHUNK_PASSES, PAIR, P], F32, tag="tp")
-            for g in range(CHUNK_PASSES):
-                for u in range(PAIR):
-                    first = (g * PAIR + u) * P
-                    nc.tensor.transpose(a_ps[:, g, u, :], words[:, first : first + P], ident[:])
-            transposed.append(a_ps)
+            banks = []
+            for word in range(0, (last - first) // PAIR, BANK_PASSES * PAIR * P):
+                passes = min(BANK_PASSES, (last - first) // K_PASS - word // (PAIR * P))
+                a_ps = psum_t.tile([P, passes, PAIR, P], F32, tag="tp")
+                for g in range(passes):
+                    for u in range(PAIR):
+                        at = word + (g * PAIR + u) * P
+                        nc.tensor.transpose(a_ps[:, g, u, :], words[:, at : at + P], ident[:])
+                banks.append(a_ps)
+            transposed[k] = banks
 
         def group_words(k):
-            grouped = grouped_pool.tile([P, CHUNK_PASSES, P, PACK], BF16, align_bytes=64)
+            first, last = columns_of(k)
+            grouped = grouped_pool.tile([P, (last - first) // K_PASS, P, PACK], BF16, align_bytes=64)
             grouped_words = grouped[:].rearrange("p g i t -> p (g i t)").bitcast(F32)
-            nc.scalar.copy(
-                out=grouped_words.rearrange("p (g i u) -> p g i u", i=P, u=PAIR),
-                in_=transposed[k][:].rearrange("p g u i -> p g i u"),
-            )
-            grouped_tiles.append(grouped)
+            for b, a_ps in enumerate(transposed[k]):
+                width = min(BANK_PASSES, (last - first) // K_PASS - b * BANK_PASSES) * PAIR * P
+                nc.scalar.copy(
+                    out=grouped_words[:, b * BANK_PASSES * PAIR * P :][:, :width].rearrange(
+                        "p (g i u) -> p g i u", i=P, u=PAIR
+                    ),
+                    in_=a_ps[:].rearrange("p g u i -> p g i u"),
+                )
+            grouped_tiles[k] = grouped
 
         def quantise(k):
-            a_codes = codes_pool.tile([P, CHUNK_PASSES, P], U32, align_bytes=64)
-            a_scales = codes_pool.tile([P, CHUNK_PASSES, P], U8, align_bytes=64)
+            r, c, end = order[k]
+            first, last = columns_of(k)
+            passes = (last - first) // K_PASS
+            a_codes = codes_pool.tile([P, passes, P], U32, align_bytes=64)
+            a_scales = codes_pool.tile([P, passes, P], U8, align_bytes=64)
             nc.vector.quantize_mx(
                 out=a_codes[:].rearrange("p g i -> p (g i)").bitcast(FP8X4),
                 scales=a_scales[:].rearrange("p g i -> p (g i)"),
                 in_=grouped_tiles[k][:].rearrange("p g i t -> p (g i t)"),
             )
-            code_tiles[order[k]] = (a_codes, a_scales)
+            for g in range(passes):
+                code_tiles[(r, first // K_PASS + g)] = (a_codes[:, g, :], a_scales[:, g, :])
 
         def multiply_row_tile(r):
             bank, slot = divmod(r, TILES_PER_BANK)
@@ -207,12 +293,11 @@ def tile_gcnlayer_pb_t_kernel(tc, A1, Hn, Wout, bout, out):
                 y_ps = psum_acc.tile([P, TILES_PER_BANK, N_OUT], F32, tag="acc")
                 sum_tiles.append(y_ps)
             for z_pass in range(PASSES):
-                c, g = divmod(z_pass, CHUNK_PASSES)
-                a_codes, a_scales = code_tiles[(r, c)]
+                codes, scales = code_tiles[(r, z_pass)]
                 nc.tensor.matmul_mx(
                     out=sum_tiles[bank][:, slot, :],
-                    lhsT=a_codes[:, g, :].bitcast(FP8X4),
-                    lhsT_scale=a_scales[:, g, :],
+                    lhsT=codes.bitcast(FP8X4),
+                    lhsT_scale=scales,
                     rhs=z_codes[:, z_pass, :].bitcast(FP8X4),
                     rhs_scale=z_scales[:, z_pass, :],
                     start=(z_pass == 0),
@@ -241,167 +326,190 @@ def tile_gcnlayer_pb_t_kernel(tc, A1, Hn, Wout, bout, out):
                 out=out_tiles[:, first_tile : first_tile + TILES_PER_BANK, :], in_=result[:]
             )
 
-        def last_unit_of(k):
-            if 0 <= k < len(order) and order[k][1] == CHUNKS - 1:
-                return order[k][0]
-            return -1
+        def ends_row_tile(k, every):
+            if 0 <= k < len(order) and order[k][2] == GROUPS:
+                if order[k][0] % every == every - 1:
+                    return order[k][0]
+            return None
 
         def work_on_unit(k):
             if k + X_AHEAD < len(order):
                 fetch_unit(k + X_AHEAD)
-            if k < len(order):
+            if k < len(order) and not by_scalar(k):
                 scale_and_transpose(k)
-            if 0 <= k - COPY_LAG < len(order):
+            if 0 <= k - COPY_LAG < len(order) and not by_scalar(k - COPY_LAG):
                 group_words(k - COPY_LAG)
+            if by_scalar(k + 3):
+                scale_rows(k + 3)
+            if by_scalar(k + 2):
+                transpose_half_hat(k + 2)
+                scale_columns(k + 2, 0)
+            if by_scalar(k + 1):
+                scale_columns(k + 1, 1)
+            if by_scalar(k):
+                interleave(k)
             if 0 <= k - QUANT_LAG < len(order):
                 quantise(k - QUANT_LAG)
-            r = last_unit_of(k - MATMUL_LAG)
-            if r % TILES_PER_RUN == TILES_PER_RUN - 1 and r >= 0:
+            r = ends_row_tile(k - MATMUL_LAG, TILES_PER_RUN)
+            if r is not None:
                 for tile in range(r - TILES_PER_RUN + 1, r + 1):
                     multiply_row_tile(tile)
-            r = last_unit_of(k - YCOPY_LAG)
-            if r % TILES_PER_BANK == TILES_PER_BANK - 1 and r >= 0:
+            r = ends_row_tile(k - YCOPY_LAG, TILES_PER_BANK)
+            if r is not None:
                 copy_sums(r // TILES_PER_BANK)
-            r = last_unit_of(k - STORE_LAG)
-            if r % TILES_PER_BANK == TILES_PER_BANK - 1 and r >= 0:
+            r = ends_row_tile(k - STORE_LAG, TILES_PER_BANK)
+            if r is not None:
                 leaky_relu_and_store(r // TILES_PER_BANK)
 
         hn_tiles = []
         h_grouped_tiles = []
         z_sums = []
+        z_tiles = []
 
-        with tc.manual_schedule():
-            with tc.tile_pool(name="zstage", bufs=2) as zstage, tc.tile_pool(name="zkeep", bufs=1) as zkeep, tc.tile_pool(name="hpool", bufs=Z_AHEAD + 1) as hpool:
-
-                def load_h(g):
-                    hn = hpool.tile([P, PACK, N_FEAT], BF16)
-                    nc.sync.dma_start(
-                        out=hn[:].rearrange("m (u e) f -> m u e f", e=PAIR),
-                        in_=Hn[g * K_PASS : (g + 1) * K_PASS, :].rearrange(
-                            "(u m e) f -> m u e f", m=P, e=PAIR
-                        ),
-                    )
-                    hn_tiles.append(hn)
-
-                def transpose_h(g):
-                    words = hn_tiles[g][:].rearrange("m t f -> m (t f)").bitcast(F32)
-                    h_grouped = zstage.tile([P, PACK * P * PACK], BF16, align_bytes=64)
-                    h_words = h_grouped[:].bitcast(F32).rearrange("p (t m u) -> p t m u", m=P, u=PAIR)
-                    for half in range(2):
-                        h_ps = psum_t.tile([P, PAIR, PAIR, P], F32, tag="tp")
-                        for a in range(PAIR):
-                            for u in range(PAIR):
-                                first = ((half * PAIR + a) * PAIR + u) * P
-                                nc.tensor.transpose(h_ps[:, a, u, :], words[:, first : first + P], ident[:])
-                        nc.scalar.copy(
-                            out=h_words[:, half * PAIR : (half + 1) * PAIR, :, :],
-                            in_=h_ps[:].rearrange("p a u m -> p a m u"),
-                        )
-                    h_grouped_tiles.append(h_grouped)
-
-                def multiply_h(g):
-                    h_codes = zstage.tile([P, PACK, P], U32, align_bytes=64)
-                    h_scales = zstage.tile([P, PACK, P], U8, align_bytes=64)
-                    nc.vector.quantize_mx(
-                        out=h_codes[:].rearrange("p t m -> p (t m)").bitcast(FP8X4),
-                        scales=h_scales[:].rearrange("p t m -> p (t m)"),
-                        in_=h_grouped_tiles[g][:],
-                    )
-                    z_ps = psum_acc.tile([P, PACK, N_OUT], F32, tag="acc")
-                    for t in range(PACK):
-                        nc.tensor.matmul_mx(
-                            out=z_ps[:, t, :],
-                            lhsT=h_codes[:, t, :].bitcast(FP8X4),
-                            lhsT_scale=h_scales[:, t, :],
-                            rhs=w_codes[:].bitcast(FP8X4),
-                            rhs_scale=w_scales[:],
-                            start=True,
-                            stop=True,
-                        )
-                    z_sums.append(z_ps)
-
-                def add_bias(g):
-                    nc.vector.tensor_tensor(
-                        out=z_grouped[:, g, :, :],
-                        in0=z_sums[g][:].rearrange("p t o -> p o t"),
-                        in1=bias_bc[:].unsqueeze(2).to_broadcast([P, N_OUT, PACK]),
-                        op=ALU.add,
-                    )
-
-                load_rows(0)
-                w_raw = zkeep.tile([P, PACK, N_OUT], BF16)
-                for u in range(PAIR):
-                    nc.sync.dma_start(
-                        out=w_raw[:, PAIR * u : PAIR * (u + 1), :],
-                        in_=Wout[256 * u : 256 * (u + 1), :].rearrange("(p e) o -> p e o", e=PAIR),
-                    )
-                load_h(0)
-                load_rows(1)
-                load_h(1)
-                bias_bc = zkeep.tile([P, N_OUT], BF16)
-                nc.sync.dma_start(out=bias_bc[:], in_=bout.partition_broadcast(P))
-                load_rows(2)
-                load_rows(3)
-
-                sum_rows_vector(0)
-                w_grouped = zkeep.tile([P, N_OUT, PACK], BF16, align_bytes=64)
-                nc.vector.tensor_copy(out=w_grouped[:], in_=w_raw[:].rearrange("p t o -> p o t"))
-                w_codes = zkeep.tile([P, N_OUT], U32, align_bytes=64)
-                w_scales = zkeep.tile([P, N_OUT], U8, align_bytes=64)
-                z_grouped = zkeep.tile([P, PASSES, N_OUT, PACK], BF16, align_bytes=64)
-
-                for step in range(FIRST_UNIT_STEP):
-                    load_rows(step + ROW_AHEAD)
-                    if step + Z_AHEAD < PASSES:
-                        load_h(step + Z_AHEAD)
-                    if step == FIRST_UNIT_STEP - 1:
-                        for k in range(X_AHEAD):
-                            fetch_unit(k)
-                    if step == GROUP_TILES:
-                        d_of_rows(0)
-                    if step == GROUP_TILES + 1:
-                        d_along_columns(0)
-                    if step > 0:
-                        sum_rows_vector(step)
-                    if step < PASSES:
-                        transpose_h(step)
-                    sum_rows_scalar(step, 0)
-                    sum_rows_scalar(step, 1)
-                    if step == 1:
-                        nc.vector.quantize_mx(
-                            out=w_codes[:].bitcast(FP8X4),
-                            scales=w_scales[:],
-                            in_=w_grouped[:].rearrange("p o t -> p (o t)"),
-                        )
-                    if 0 <= step - 1 < PASSES:
-                        multiply_h(step - 1)
-                    if 0 <= step - 2 < PASSES:
-                        add_bias(step - 2)
-                nc.vector.quantize_mx(
-                    out=z_codes[:].rearrange("p g o -> p (g o)").bitcast(FP8X4),
-                    scales=z_scales[:].rearrange("p g o -> p (g o)"),
-                    in_=z_grouped[:].rearrange("p g o t -> p (g o t)"),
+        def load_w():
+            for u in range(PAIR):
+                nc.sync.dma_start(
+                    out=w_raw[:, PAIR * u : PAIR * (u + 1), :],
+                    in_=Wout[256 * u : 256 * (u + 1), :].rearrange("(p e) o -> p e o", e=PAIR),
                 )
 
-            codes_pool = ctx.enter_context(tc.tile_pool(name="codes_pool", bufs=84))
-            k = 0
-            for step in range(FIRST_UNIT_STEP, ROW_TILES + D_LAG):
+        def load_h(g):
+            hn = hpool.tile([P, PACK, N_FEAT], BF16)
+            nc.sync.dma_start(
+                out=hn[:].rearrange("m (u e) f -> m u e f", e=PAIR),
+                in_=Hn[g * K_PASS : (g + 1) * K_PASS, :].rearrange("(u m e) f -> m u e f", m=P, e=PAIR),
+            )
+            hn_tiles.append(hn)
+
+        def transpose_h(g):
+            words = hn_tiles[g][:].rearrange("m t f -> m (t f)").bitcast(F32)
+            h_grouped = zstage.tile([P, PACK * P * PACK], BF16, align_bytes=64)
+            h_words = h_grouped[:].bitcast(F32).rearrange("p (t m u) -> p t m u", m=P, u=PAIR)
+            for half in range(2):
+                h_ps = psum_t.tile([P, PAIR, PAIR, P], F32, tag="tp")
+                for a in range(PAIR):
+                    for u in range(PAIR):
+                        first = ((half * PAIR + a) * PAIR + u) * P
+                        nc.tensor.transpose(h_ps[:, a, u, :], words[:, first : first + P], ident[:])
+                nc.scalar.copy(
+                    out=h_words[:, half * PAIR : (half + 1) * PAIR, :, :],
+                    in_=h_ps[:].rearrange("p a u m -> p a m u"),
+                )
+            h_grouped_tiles.append(h_grouped)
+
+        def multiply_h(g):
+            h_codes = zstage.tile([P, PACK, P], U32, align_bytes=64)
+            h_scales = zstage.tile([P, PACK, P], U8, align_bytes=64)
+            nc.vector.quantize_mx(
+                out=h_codes[:].rearrange("p t m -> p (t m)").bitcast(FP8X4),
+                scales=h_scales[:].rearrange("p t m -> p (t m)"),
+                in_=h_grouped_tiles[g][:],
+            )
+            z_ps = psum_acc.tile([P, PACK, N_OUT], F32, tag="acc")
+            for t in range(PACK):
+                nc.tensor.matmul_mx(
+                    out=z_ps[:, t, :],
+                    lhsT=h_codes[:, t, :].bitcast(FP8X4),
+                    lhsT_scale=h_scales[:, t, :],
+                    rhs=w_codes[:].bitcast(FP8X4),
+                    rhs_scale=w_scales[:],
+                    start=True,
+                    stop=True,
+                )
+            z_sums.append(z_ps)
+
+        def add_bias(g):
+            z_grouped = zstage.tile([P, N_OUT, PACK], BF16, align_bytes=64)
+            nc.vector.tensor_tensor(
+                out=z_grouped[:],
+                in0=z_sums[g][:].rearrange("p t o -> p o t"),
+                in1=bias_bc[:].unsqueeze(2).to_broadcast([P, N_OUT, PACK]),
+                op=ALU.add,
+            )
+            z_tiles.append(z_grouped)
+
+        def quantise_z(g):
+            nc.vector.quantize_mx(
+                out=z_codes[:, g, :].bitcast(FP8X4),
+                scales=z_scales[:, g, :],
+                in_=z_tiles[g][:].rearrange("p o t -> p (o t)"),
+            )
+
+        def work_on_z(z):
+            if z == 0:
+                nc.vector.tensor_copy(out=w_grouped[:], in_=w_raw[:].rearrange("p t o -> p o t"))
+            if 0 <= z < PASSES:
+                transpose_h(z)
+            if z == 1:
+                nc.vector.quantize_mx(
+                    out=w_codes[:].bitcast(FP8X4),
+                    scales=w_scales[:],
+                    in_=w_grouped[:].rearrange("p o t -> p (o t)"),
+                )
+            if 0 <= z - 1 < PASSES:
+                multiply_h(z - 1)
+            if 0 <= z - 2 < PASSES:
+                add_bias(z - 2)
+            if 0 <= z - 3 < PASSES:
+                quantise_z(z - 3)
+
+        def run_steps(first_step, last_step, k):
+            for step in range(first_step, last_step):
                 if step + ROW_AHEAD < ROW_TILES:
                     load_rows(step + ROW_AHEAD)
-                q, s = divmod(step, GROUP_TILES)
-                if s == 0:
-                    d_of_rows(q - 1)
-                if s == 1:
-                    d_along_columns(q - 1)
+                z = step - Z_FIRST
+                if z + Z_AHEAD == 0:
+                    load_w()
+                if z + Z_AHEAD == 1:
+                    nc.sync.dma_start(out=bias_bc[:], in_=bout.partition_broadcast(P))
+                if 0 <= z + Z_AHEAD < PASSES:
+                    load_h(z + Z_AHEAD)
+                if step == FIRST_TILE[1] + D_LAG - 1:
+                    for ahead in range(X_AHEAD):
+                        fetch_unit(ahead)
+                if step < 0:
+                    continue
+                late = []
+                for q in range(GROUPS):
+                    s = step - FIRST_TILE[q + 1]
+                    if s == 0:
+                        late = [add_row_sums]
+                    if s == 1:
+                        late = [square_guess, half_product, d_of_rows]
+                    if s == D_LAG - 1:
+                        late.append(d_along_columns)
+                    if late:
+                        break
                 if step < ROW_TILES:
                     sum_rows_vector(step)
-                    sum_rows_scalar(step, 0)
+                work_on_z(z)
                 count = units_at_step(step)
                 for i in range(count):
                     work_on_unit(k)
                     k += 1
-                    if i == count // 2 and step < ROW_TILES:
-                        sum_rows_scalar(step, 1)
+                    if i == 0 and step < ROW_TILES:
+                        sum_rows_scalar(step)
+                    for small in late[i : i + 1]:
+                        small(q)
+                if count == 0 and step < ROW_TILES:
+                    sum_rows_scalar(step)
+                for small in late[count:]:
+                    small(q)
+            return k
+
+        with tc.manual_schedule():
+            with tc.tile_pool(name="zkeep", bufs=1) as zkeep, tc.tile_pool(name="zstage", bufs=2) as zstage, tc.tile_pool(name="hpool", bufs=Z_AHEAD + 1) as hpool:
+                w_raw = zkeep.tile([P, PACK, N_OUT], BF16)
+                bias_bc = zkeep.tile([P, N_OUT], BF16)
+                w_grouped = zkeep.tile([P, N_OUT, PACK], BF16, align_bytes=64)
+                w_codes = zkeep.tile([P, N_OUT], U32, align_bytes=64)
+                w_scales = zkeep.tile([P, N_OUT], U8, align_bytes=64)
+                k = run_steps(-ROW_AHEAD, Z_LAST, 0)
+            offload_pool = ctx.enter_context(tc.tile_pool(name="offload_pool", bufs=2))
+            ypool = ctx.enter_context(tc.tile_pool(name="ypool", bufs=2))
+            k = run_steps(Z_LAST, ROW_TILES + D_LAG, k)
+            for g in range(PASSES):
+                d_along_words(g)
             while k < len(order) + STORE_LAG:
                 work_on_unit(k)
                 k += 1

@@ -23,29 +23,30 @@ LEAKY_SLOPE = 0.01
 ROW_TILES = N_NODES // P
 PASSES = N_NODES // K_PASS
 GROUP_TILES = (8, 8, 8, 8)
-VECTOR_SUM_COLS = (2688, 2304, 1280, 1024)
+VECTOR_SUM_COLS = (3072, 2560, 1280, 768)
 GROUPS = len(GROUP_TILES)
 FIRST_TILE = [sum(GROUP_TILES[:q]) for q in range(GROUPS + 1)]
 GROUP_OF = [q for q in range(GROUPS) for r in range(GROUP_TILES[q])]
 TILES_PER_BANK = 4
 TILES_PER_RUN = 2
 
-ROW_AHEAD = 4
+ROW_AHEAD = 3
 Z_AHEAD = 2
-X_AHEAD = 7
+X_AHEAD = 3
 COPY_LAG = 1
-QUANT_LAG = 4
-MATMUL_LAG = 5
-YCOPY_LAG = 6
-STORE_LAG = 9
-OFFLOAD_LEAD = 3
-D_LAG = 2
+QUANT_LAG = 2
+MATMUL_LAG = 3
+YCOPY_LAG = 4
+STORE_LAG = 6
+OFFLOAD_LEAD = 2
+FETCH_STEP = 7
+D_LAG = 1
 Z_FIRST = 0
 Z_LAST = Z_FIRST + PASSES + 3
-UNIT_CHUNKS = 1
-CODES_BUFS = 84
-OFFLOAD_EVERY = 4
-BANK_PASSES = 2
+CHUNK = 1024
+CHUNK_PASSES = CHUNK // K_PASS
+CODES_BUFS = 42
+OFFLOAD_EVERY = (0, 0, 0, 4)
 
 FLOPS = 2 * N_NODES * N_FEAT * N_OUT + 2 * N_NODES * N_NODES * N_OUT
 
@@ -56,7 +57,7 @@ def tile_gcnlayer_pb_t_kernel(tc, A1, Hn, Wout, bout, out):
         keep = ctx.enter_context(tc.tile_pool(name="keep", bufs=1))
         rowpool = ctx.enter_context(tc.tile_pool(name="rowpool", bufs=ROW_AHEAD + 1))
         xpool = ctx.enter_context(tc.tile_pool(name="xpool", bufs=X_AHEAD + 2))
-        hat_pool = ctx.enter_context(tc.tile_pool(name="hat_pool", bufs=3))
+        hat_pool = ctx.enter_context(tc.tile_pool(name="hat_pool", bufs=2))
         grouped_pool = ctx.enter_context(tc.tile_pool(name="grouped_pool", bufs=QUANT_LAG + 2))
         dpool = ctx.enter_context(tc.tile_pool(name="dpool", bufs=2))
         codes_pool = ctx.enter_context(tc.tile_pool(name="codes_pool", bufs=CODES_BUFS))
@@ -146,13 +147,25 @@ def tile_gcnlayer_pb_t_kernel(tc, A1, Hn, Wout, bout, out):
                     in_=d_ps[:].rearrange("p a n -> p (a n)"),
                 )
 
+        def d_of_chunk(q):
+            d_along_columns(q)
+            for g in range(FIRST_TILE[q] // PACK, FIRST_TILE[q + 1] // PACK):
+                d_along_words(g)
+
         by_group = []
         for q in range(GROUPS):
-            fresh = [(r, q, q + 1) for r in range(FIRST_TILE[q])]
-            for r in range(FIRST_TILE[q], FIRST_TILE[q + 1]):
-                fresh.extend([(r, c, min(c + UNIT_CHUNKS, q + 1)) for c in range(0, q + 1, UNIT_CHUNKS)])
+            fresh = [((r, q), (r + 1, q)) for r in range(0, FIRST_TILE[q], 2)]
+            wide = (q + 1) // 2 * 2
+            for r in range(FIRST_TILE[q], FIRST_TILE[q + 1], 2):
+                for tile in (r, r + 1):
+                    fresh.extend([((tile, c), (tile, c + 1)) for c in range(0, wide, 2)])
+                if wide <= q:
+                    fresh.append(((r, q), (r + 1, q)))
             by_group.append(fresh)
         order = [unit for fresh in by_group for unit in fresh]
+
+        def one_row_tile(k):
+            return order[k][0][0] == order[k][1][0]
 
         def units_at_step(step):
             for q in range(GROUPS - 1):
@@ -162,69 +175,76 @@ def tile_gcnlayer_pb_t_kernel(tc, A1, Hn, Wout, bout, out):
                     return len(by_group[q]) * (s + 1) // n - len(by_group[q]) * s // n
             return 0
 
-        def columns_of(k):
-            r, c, end = order[k]
-            return FIRST_TILE[c] * P, FIRST_TILE[end] * P
-
         x_tiles = []
         grouped_tiles = {}
+        hat_tiles = {}
         transposed = {}
         code_tiles = {}
         sum_tiles = []
         copy_tiles = []
 
         def fetch_unit(k):
-            r = order[k][0]
-            first, last = columns_of(k)
-            x = xpool.tile([P, last - first], BF16)
-            nc.sync.dma_start(out=x[:], in_=A1[r * P : (r + 1) * P, first:last])
+            r, c = order[k][0]
+            x = xpool.tile([P, 2, CHUNK], BF16)
+            if one_row_tile(k):
+                source = A1[r * P : (r + 1) * P, c * CHUNK : (c + 2) * CHUNK].rearrange(
+                    "p (b j) -> p b j", b=2
+                )
+            else:
+                source = A1[r * P : (r + 2) * P, c * CHUNK : (c + 1) * CHUNK].rearrange(
+                    "(b p) j -> p b j", b=2
+                )
+            nc.sync.dma_start(out=x[:], in_=source)
             x_tiles.append(x)
 
         def by_scalar(k):
-            first_late = len(order) - len(by_group[-1])
-            return first_late + OFFLOAD_LEAD <= k < len(order) - OFFLOAD_LEAD and (k - first_late) % OFFLOAD_EVERY == OFFLOAD_EVERY - 1
+            if not 0 <= k < len(order) - OFFLOAD_LEAD:
+                return False
+            start = 0
+            for q in range(GROUPS):
+                if k < start + len(by_group[q]):
+                    every = OFFLOAD_EVERY[q]
+                    at = k - start
+                    return every > 0 and at >= OFFLOAD_LEAD and at % every == every - 1
+                start += len(by_group[q])
 
         scaled_rows = {}
-        scaled_banks = {}
         scaled_columns = {}
 
         def scale_rows(k):
-            r = order[k][0]
-            first, last = columns_of(k)
-            half_hat = offload_pool.tile([P, last - first], F32)
-            nc.scalar.activation(out=half_hat[:], in_=x_tiles[k][:], func=ACT.Copy, scale=d_rows[:, r : r + 1])
+            half_hat = offload_pool.tile([P, 2, CHUNK // (PAIR * P), PAIR, P], F32)
+            for b, (r, c) in enumerate(order[k]):
+                nc.scalar.activation(
+                    out=half_hat[:, b, :, :, :],
+                    in_=x_tiles[k][:, b, :].rearrange("i (w p e) -> i w e p", p=P, e=PAIR),
+                    func=ACT.Copy,
+                    scale=d_rows[:, r : r + 1],
+                )
             scaled_rows[k] = half_hat
 
-        def transpose_half_hat(k):
-            first, last = columns_of(k)
-            banks = []
-            for g in range((last - first) // K_PASS):
+        def scale_columns(k, b):
+            if b == 0:
+                hat_columns = offload_pool.tile([P, 2, CHUNK_PASSES, PACK, P], BF16)
+                scaled_columns[k] = hat_columns
+            for g in range(CHUNK_PASSES):
                 t_ps = psum_t.tile([P, PACK, P], F32, tag="tp")
                 for t in range(PACK):
                     u, e = divmod(t, PAIR)
-                    at = (g * PAIR + u) * PAIR * P + e
-                    nc.tensor.transpose(t_ps[:, t, :], scaled_rows[k][:, at : at + PAIR * P - 1 : PAIR], ident[:])
-                banks.append(t_ps)
-            scaled_banks[k] = banks
-
-        def scale_columns(k, g):
-            first, last = columns_of(k)
-            if g == 0:
-                hat_columns = offload_pool.tile([P, (last - first) // K_PASS, PACK, P], BF16)
-                scaled_columns[k] = hat_columns
-            for t in range(PACK):
-                at = first // P + g * PACK + t
-                nc.scalar.activation(
-                    out=scaled_columns[k][:, g, t, :],
-                    in_=scaled_banks[k][g][:, t, :],
-                    func=ACT.Copy,
-                    scale=d_words[:, at : at + 1],
-                )
+                    nc.tensor.transpose(t_ps[:, t, :], scaled_rows[k][:, b, g * PAIR + u, e, :], ident[:])
+                for t in range(PACK):
+                    at = (order[k][b][1] * CHUNK_PASSES + g) * PACK + t
+                    nc.scalar.activation(
+                        out=scaled_columns[k][:, b, g, t, :],
+                        in_=t_ps[:, t, :],
+                        func=ACT.Copy,
+                        scale=d_words[:, at : at + 1],
+                    )
 
         def interleave(k):
-            first, last = columns_of(k)
-            grouped = grouped_pool.tile([P, (last - first) // K_PASS, P, PACK], BF16, align_bytes=64)
-            nc.scalar.copy(out=grouped[:], in_=scaled_columns[k][:].rearrange("p g t i -> p g i t"))
+            grouped = grouped_pool.tile([P, 2 * CHUNK_PASSES, P, PACK], BF16, align_bytes=64)
+            nc.scalar.copy(
+                out=grouped[:], in_=scaled_columns[k][:].rearrange("p b g t i -> p (b g) i t")
+            )
             grouped_tiles[k] = grouped
 
         def d_along_words(g):
@@ -235,57 +255,55 @@ def tile_gcnlayer_pb_t_kernel(tc, A1, Hn, Wout, bout, out):
                 nc.tensor.transpose(d_ps[:, t, :], d_cols[:, at : at + PAIR * P - 1 : PAIR], ident[:])
             nc.scalar.copy(out=d_words[:, g * PACK : (g + 1) * PACK], in_=d_ps[:, :, 0])
 
-        def scale_and_transpose(k):
-            r = order[k][0]
-            first, last = columns_of(k)
-            a_hat = hat_pool.tile([P, last - first], BF16)
+        def scale_blocks(k, b):
+            if b == 0:
+                a_hat = hat_pool.tile([P, 2, CHUNK], BF16)
+                hat_tiles[k] = a_hat
+            elif one_row_tile(k):
+                return
+            n = 2 if one_row_tile(k) else 1
+            r, c = order[k][b]
             nc.vector.scalar_tensor_tensor(
-                out=a_hat[:],
-                in0=x_tiles[k][:],
+                out=hat_tiles[k][:, b : b + n, :].rearrange("p b j -> p (b j)"),
+                in0=x_tiles[k][:, b : b + n, :].rearrange("p b j -> p (b j)"),
                 scalar=d_rows[:, r : r + 1],
-                in1=d_cols[:, first:last],
+                in1=d_cols[:, c * CHUNK : (c + n) * CHUNK],
                 op0=ALU.mult,
                 op1=ALU.mult,
             )
-            words = a_hat[:].bitcast(F32)
-            banks = []
-            for word in range(0, (last - first) // PAIR, BANK_PASSES * PAIR * P):
-                passes = min(BANK_PASSES, (last - first) // K_PASS - word // (PAIR * P))
-                a_ps = psum_t.tile([P, passes, PAIR, P], F32, tag="tp")
-                for g in range(passes):
-                    for u in range(PAIR):
-                        at = word + (g * PAIR + u) * P
-                        nc.tensor.transpose(a_ps[:, g, u, :], words[:, at : at + P], ident[:])
-                banks.append(a_ps)
-            transposed[k] = banks
 
-        def group_words(k):
-            first, last = columns_of(k)
-            grouped = grouped_pool.tile([P, (last - first) // K_PASS, P, PACK], BF16, align_bytes=64)
-            grouped_words = grouped[:].rearrange("p g i t -> p (g i t)").bitcast(F32)
-            for b, a_ps in enumerate(transposed[k]):
-                width = min(BANK_PASSES, (last - first) // K_PASS - b * BANK_PASSES) * PAIR * P
-                nc.scalar.copy(
-                    out=grouped_words[:, b * BANK_PASSES * PAIR * P :][:, :width].rearrange(
-                        "p (g i u) -> p g i u", i=P, u=PAIR
-                    ),
-                    in_=a_ps[:].rearrange("p g u i -> p g i u"),
-                )
-            grouped_tiles[k] = grouped
+        def transpose_block(k, b):
+            words = hat_tiles[k][:, b, :].bitcast(F32)
+            a_ps = psum_t.tile([P, CHUNK_PASSES, PAIR, P], F32, tag="tp")
+            for g in range(CHUNK_PASSES):
+                for u in range(PAIR):
+                    at = (g * PAIR + u) * P
+                    nc.tensor.transpose(a_ps[:, g, u, :], words[:, at : at + P], ident[:])
+            transposed[(k, b)] = a_ps
+
+        def group_words(k, b):
+            if b == 0:
+                grouped = grouped_pool.tile([P, 2 * CHUNK_PASSES, P, PACK], BF16, align_bytes=64)
+                grouped_tiles[k] = grouped
+            words = grouped_tiles[k][:].rearrange("p g i t -> p (g i t)").bitcast(F32)
+            n = CHUNK // PAIR
+            nc.scalar.copy(
+                out=words[:, b * n : (b + 1) * n].rearrange("p (g i u) -> p g i u", i=P, u=PAIR),
+                in_=transposed[(k, b)][:].rearrange("p g u i -> p g i u"),
+            )
 
         def quantise(k):
-            r, c, end = order[k]
-            first, last = columns_of(k)
-            passes = (last - first) // K_PASS
-            a_codes = codes_pool.tile([P, passes, P], U32, align_bytes=64)
-            a_scales = codes_pool.tile([P, passes, P], U8, align_bytes=64)
+            a_codes = codes_pool.tile([P, 2 * CHUNK_PASSES, P], U32, align_bytes=64)
+            a_scales = codes_pool.tile([P, 2 * CHUNK_PASSES, P], U8, align_bytes=64)
             nc.vector.quantize_mx(
                 out=a_codes[:].rearrange("p g i -> p (g i)").bitcast(FP8X4),
                 scales=a_scales[:].rearrange("p g i -> p (g i)"),
                 in_=grouped_tiles[k][:].rearrange("p g i t -> p (g i t)"),
             )
-            for g in range(passes):
-                code_tiles[(r, first // K_PASS + g)] = (a_codes[:, g, :], a_scales[:, g, :])
+            for b, (r, c) in enumerate(order[k]):
+                for g in range(CHUNK_PASSES):
+                    at = b * CHUNK_PASSES + g
+                    code_tiles[(r, c * CHUNK_PASSES + g)] = (a_codes[:, at, :], a_scales[:, at, :])
 
         def multiply_row_tile(r):
             bank, slot = divmod(r, TILES_PER_BANK)
@@ -327,29 +345,31 @@ def tile_gcnlayer_pb_t_kernel(tc, A1, Hn, Wout, bout, out):
             )
 
         def ends_row_tile(k, every):
-            if 0 <= k < len(order) and order[k][2] == GROUPS:
-                if order[k][0] % every == every - 1:
-                    return order[k][0]
+            if 0 <= k < len(order):
+                r, c = order[k][1]
+                if c == GROUPS - 1 and r % every == every - 1:
+                    return r
             return None
 
         def work_on_unit(k):
             if k + X_AHEAD < len(order):
                 fetch_unit(k + X_AHEAD)
-            if k < len(order) and not by_scalar(k):
-                scale_and_transpose(k)
-            if 0 <= k - COPY_LAG < len(order) and not by_scalar(k - COPY_LAG):
-                group_words(k - COPY_LAG)
-            if by_scalar(k + 3):
-                scale_rows(k + 3)
             if by_scalar(k + 2):
-                transpose_half_hat(k + 2)
-                scale_columns(k + 2, 0)
-            if by_scalar(k + 1):
-                scale_columns(k + 1, 1)
-            if by_scalar(k):
-                interleave(k)
-            if 0 <= k - QUANT_LAG < len(order):
-                quantise(k - QUANT_LAG)
+                scale_rows(k + 2)
+            for b in range(2):
+                if k < len(order) and not by_scalar(k):
+                    scale_blocks(k, b)
+                    transpose_block(k, b)
+                done = k - 1 + b
+                if 0 <= done < len(order) and not by_scalar(done):
+                    group_words(done, 1 - b)
+                if by_scalar(k + 1):
+                    scale_columns(k + 1, b)
+                if b == 0:
+                    if by_scalar(k):
+                        interleave(k)
+                    if 0 <= k - QUANT_LAG < len(order):
+                        quantise(k - QUANT_LAG)
             r = ends_row_tile(k - MATMUL_LAG, TILES_PER_RUN)
             if r is not None:
                 for tile in range(r - TILES_PER_RUN + 1, r + 1):
@@ -464,7 +484,7 @@ def tile_gcnlayer_pb_t_kernel(tc, A1, Hn, Wout, bout, out):
                     nc.sync.dma_start(out=bias_bc[:], in_=bout.partition_broadcast(P))
                 if 0 <= z + Z_AHEAD < PASSES:
                     load_h(z + Z_AHEAD)
-                if step == FIRST_TILE[1] + D_LAG - 1:
+                if step == FETCH_STEP:
                     for ahead in range(X_AHEAD):
                         fetch_unit(ahead)
                 if step < 0:
@@ -473,11 +493,7 @@ def tile_gcnlayer_pb_t_kernel(tc, A1, Hn, Wout, bout, out):
                 for q in range(GROUPS):
                     s = step - FIRST_TILE[q + 1]
                     if s == 0:
-                        late = [add_row_sums]
-                    if s == 1:
-                        late = [square_guess, half_product, d_of_rows]
-                    if s == D_LAG - 1:
-                        late.append(d_along_columns)
+                        late = [add_row_sums, square_guess, half_product, d_of_rows, d_of_chunk]
                     if late:
                         break
                 if step < ROW_TILES:
@@ -508,8 +524,6 @@ def tile_gcnlayer_pb_t_kernel(tc, A1, Hn, Wout, bout, out):
             offload_pool = ctx.enter_context(tc.tile_pool(name="offload_pool", bufs=2))
             ypool = ctx.enter_context(tc.tile_pool(name="ypool", bufs=2))
             k = run_steps(Z_LAST, ROW_TILES + D_LAG, k)
-            for g in range(PASSES):
-                d_along_words(g)
             while k < len(order) + STORE_LAG:
                 work_on_unit(k)
                 k += 1

@@ -513,17 +513,16 @@ def tile_gcnlayer_pb_t_kernel(tc, A1, Hn, Wout, bout, out):
                     small(q)
             return k
 
-        with tc.manual_schedule():
-            with tc.tile_pool(name="zkeep", bufs=1) as zkeep, tc.tile_pool(name="zstage", bufs=2) as zstage, tc.tile_pool(name="hpool", bufs=Z_AHEAD + 1) as hpool:
-                w_raw = zkeep.tile([P, PACK, N_OUT], BF16)
-                bias_bc = zkeep.tile([P, N_OUT], BF16)
-                w_grouped = zkeep.tile([P, N_OUT, PACK], BF16, align_bytes=64)
-                w_codes = zkeep.tile([P, N_OUT], U32, align_bytes=64)
-                w_scales = zkeep.tile([P, N_OUT], U8, align_bytes=64)
-                k = run_steps(-ROW_AHEAD, Z_LAST, 0)
-            offload_pool = ctx.enter_context(tc.tile_pool(name="offload_pool", bufs=2))
-            ypool = ctx.enter_context(tc.tile_pool(name="ypool", bufs=2))
-            k = run_steps(Z_LAST, ROW_TILES + D_LAG, k)
-            while k < len(order) + STORE_LAG:
-                work_on_unit(k)
-                k += 1
+        with tc.tile_pool(name="zkeep", bufs=1) as zkeep, tc.tile_pool(name="zstage", bufs=2) as zstage, tc.tile_pool(name="hpool", bufs=Z_AHEAD + 1) as hpool:
+            w_raw = zkeep.tile([P, PACK, N_OUT], BF16)
+            bias_bc = zkeep.tile([P, N_OUT], BF16)
+            w_grouped = zkeep.tile([P, N_OUT, PACK], BF16, align_bytes=64)
+            w_codes = zkeep.tile([P, N_OUT], U32, align_bytes=64)
+            w_scales = zkeep.tile([P, N_OUT], U8, align_bytes=64)
+            k = run_steps(-ROW_AHEAD, Z_LAST, 0)
+        offload_pool = ctx.enter_context(tc.tile_pool(name="offload_pool", bufs=2))
+        ypool = ctx.enter_context(tc.tile_pool(name="ypool", bufs=2))
+        k = run_steps(Z_LAST, ROW_TILES + D_LAG, k)
+        while k < len(order) + STORE_LAG:
+            work_on_unit(k)
+            k += 1

@@ -22,15 +22,14 @@ LEAKY_SLOPE = 0.01
 
 ROW_TILES = N_NODES // P
 PASSES = N_NODES // K_PASS
-GROUP_TILES = (8, 8, 8, 8)
-VECTOR_SUM_COLS = (3072, 2560, 1280, 768)
+GROUP_TILES = (4, 4, 8, 8, 8)
+VECTOR_SUM_COLS = (3072, 3072, 2304, 1536, 256)
 GROUPS = len(GROUP_TILES)
 FIRST_TILE = [sum(GROUP_TILES[:q]) for q in range(GROUPS + 1)]
 GROUP_OF = [q for q in range(GROUPS) for r in range(GROUP_TILES[q])]
 TILES_PER_BANK = 4
-TILES_PER_RUN = 2
 
-ROW_AHEAD = 3
+ROW_AHEAD = 4
 Z_AHEAD = 2
 X_AHEAD = 3
 COPY_LAG = 1
@@ -39,14 +38,39 @@ MATMUL_LAG = 3
 YCOPY_LAG = 4
 STORE_LAG = 6
 OFFLOAD_LEAD = 2
-FETCH_STEP = 7
-D_LAG = 1
+FETCH_STEP = 3
+EARLY_OFFLOADS = 0
+D_LAG = 2
 Z_FIRST = 0
 Z_LAST = Z_FIRST + PASSES + 3
-CHUNK = 1024
-CHUNK_PASSES = CHUNK // K_PASS
-CODES_BUFS = 42
-OFFLOAD_EVERY = (0, 0, 0, 4)
+UNIT_PASSES = 4
+CODES_BUFS = 41
+OFFLOAD_EVERY = 2
+
+
+def mixed(units):
+    several = [unit for unit in units if unit[1] > 1]
+    single = [unit for unit in units if unit[1] == 1]
+    result = []
+    taken = 0
+    for i in range(len(units)):
+        if taken < len(several) and taken * len(units) <= i * len(several):
+            result.append(several[taken])
+            taken += 1
+        else:
+            result.append(single[i - taken])
+    return result
+
+
+def scalar_units_of(order, by_group):
+    first_late = len(order) - len(by_group[-1])
+    several = [k for k in range(first_late, len(order)) if order[k][1] > 1]
+    units = several[OFFLOAD_EVERY - 1 :: OFFLOAD_EVERY]
+    first = first_late - len(by_group[-2])
+    several = [k for k in range(first, first_late) if order[k][1] > 1]
+    units.extend(several[len(several) - EARLY_OFFLOADS :])
+    return set(units)
+
 
 FLOPS = 2 * N_NODES * N_FEAT * N_OUT + 2 * N_NODES * N_NODES * N_OUT
 
@@ -152,20 +176,25 @@ def tile_gcnlayer_pb_t_kernel(tc, A1, Hn, Wout, bout, out):
             for g in range(FIRST_TILE[q] // PACK, FIRST_TILE[q + 1] // PACK):
                 d_along_words(g)
 
+        def rectangles(r, r_end, g, g_end):
+            units = []
+            for m in (4, 2, 1):
+                n = UNIT_PASSES // m
+                while g_end - g >= m:
+                    units.extend([(first, n, g, m) for first in range(r, r_end, n)])
+                    g += m
+            return units
+
         by_group = []
         for q in range(GROUPS):
-            fresh = [((r, q), (r + 1, q)) for r in range(0, FIRST_TILE[q], 2)]
-            wide = (q + 1) // 2 * 2
-            for r in range(FIRST_TILE[q], FIRST_TILE[q + 1], 2):
-                for tile in (r, r + 1):
-                    fresh.extend([((tile, c), (tile, c + 1)) for c in range(0, wide, 2)])
-                if wide <= q:
-                    fresh.append(((r, q), (r + 1, q)))
+            first, last = FIRST_TILE[q], FIRST_TILE[q + 1]
+            fresh = rectangles(0, first, first // PACK, last // PACK)
+            fresh.extend(rectangles(first, last, 0, last // PACK))
             by_group.append(fresh)
+        by_group[-1] = mixed(by_group[-1])
+        by_group[-2] = mixed(by_group[-2])
         order = [unit for fresh in by_group for unit in fresh]
-
-        def one_row_tile(k):
-            return order[k][0][0] == order[k][1][0]
+        scalar_units = scalar_units_of(order, by_group)
 
         def units_at_step(step):
             for q in range(GROUPS - 1):
@@ -180,70 +209,66 @@ def tile_gcnlayer_pb_t_kernel(tc, A1, Hn, Wout, bout, out):
         hat_tiles = {}
         transposed = {}
         code_tiles = {}
-        sum_tiles = []
-        copy_tiles = []
+        sum_tiles = {}
+        copy_tiles = {}
 
         def fetch_unit(k):
-            r, c = order[k][0]
-            x = xpool.tile([P, 2, CHUNK], BF16)
-            if one_row_tile(k):
-                source = A1[r * P : (r + 1) * P, c * CHUNK : (c + 2) * CHUNK].rearrange(
-                    "p (b j) -> p b j", b=2
-                )
-            else:
-                source = A1[r * P : (r + 2) * P, c * CHUNK : (c + 1) * CHUNK].rearrange(
-                    "(b p) j -> p b j", b=2
-                )
-            nc.sync.dma_start(out=x[:], in_=source)
+            r, n, g, m = order[k]
+            x = xpool.tile([P, n, m * K_PASS], BF16)
+            nc.sync.dma_start(
+                out=x[:],
+                in_=A1[r * P : (r + n) * P, g * K_PASS : (g + m) * K_PASS].rearrange(
+                    "(b p) j -> p b j", p=P
+                ),
+            )
             x_tiles.append(x)
 
         def by_scalar(k):
-            if not 0 <= k < len(order) - OFFLOAD_LEAD:
-                return False
-            start = 0
-            for q in range(GROUPS):
-                if k < start + len(by_group[q]):
-                    every = OFFLOAD_EVERY[q]
-                    at = k - start
-                    return every > 0 and at >= OFFLOAD_LEAD and at % every == every - 1
-                start += len(by_group[q])
+            return k in scalar_units
 
         scaled_rows = {}
         scaled_columns = {}
 
         def scale_rows(k):
-            half_hat = offload_pool.tile([P, 2, CHUNK // (PAIR * P), PAIR, P], F32)
-            for b, (r, c) in enumerate(order[k]):
+            r, n, g, m = order[k]
+            half_hat = offload_pool.tile([P, n, m * PAIR, PAIR, P], F32)
+            for b in range(n):
                 nc.scalar.activation(
                     out=half_hat[:, b, :, :, :],
                     in_=x_tiles[k][:, b, :].rearrange("i (w p e) -> i w e p", p=P, e=PAIR),
                     func=ACT.Copy,
-                    scale=d_rows[:, r : r + 1],
+                    scale=d_rows[:, r + b : r + b + 1],
                 )
             scaled_rows[k] = half_hat
+            hat_columns = offload_pool.tile([P, n, m, PACK, P], BF16)
+            scaled_columns[k] = hat_columns
 
-        def scale_columns(k, b):
-            if b == 0:
-                hat_columns = offload_pool.tile([P, 2, CHUNK_PASSES, PACK, P], BF16)
-                scaled_columns[k] = hat_columns
-            for g in range(CHUNK_PASSES):
-                t_ps = psum_t.tile([P, PACK, P], F32, tag="tp")
-                for t in range(PACK):
+        def scale_columns(k, half):
+            r, n, g, m = order[k]
+            values = [(h, t) for h in range(m) for t in range(PACK)]
+            values = values[len(values) * half // 2 : len(values) * (half + 1) // 2]
+            in_bank = TILES_PER_BANK // n
+            for first in range(0, len(values), in_bank):
+                t_ps = psum_t.tile([P, in_bank, n, P], F32, tag="tp")
+                for s in range(in_bank):
+                    h, t = values[first + s]
                     u, e = divmod(t, PAIR)
-                    nc.tensor.transpose(t_ps[:, t, :], scaled_rows[k][:, b, g * PAIR + u, e, :], ident[:])
-                for t in range(PACK):
-                    at = (order[k][b][1] * CHUNK_PASSES + g) * PACK + t
+                    for b in range(n):
+                        nc.tensor.transpose(t_ps[:, s, b, :], scaled_rows[k][:, b, h * PAIR + u, e, :], ident[:])
+                for s in range(in_bank):
+                    h, t = values[first + s]
+                    at = (g + h) * PACK + t
                     nc.scalar.activation(
-                        out=scaled_columns[k][:, b, g, t, :],
-                        in_=t_ps[:, t, :],
+                        out=scaled_columns[k][:, :, h, t, :],
+                        in_=t_ps[:, s, :, :],
                         func=ACT.Copy,
                         scale=d_words[:, at : at + 1],
                     )
 
         def interleave(k):
-            grouped = grouped_pool.tile([P, 2 * CHUNK_PASSES, P, PACK], BF16, align_bytes=64)
+            grouped = grouped_pool.tile([P, UNIT_PASSES, P, PACK], BF16, align_bytes=64)
             nc.scalar.copy(
-                out=grouped[:], in_=scaled_columns[k][:].rearrange("p b g t i -> p (b g) i t")
+                out=grouped[:], in_=scaled_columns[k][:].rearrange("p b h t i -> p (b h) i t")
             )
             grouped_tiles[k] = grouped
 
@@ -255,61 +280,60 @@ def tile_gcnlayer_pb_t_kernel(tc, A1, Hn, Wout, bout, out):
                 nc.tensor.transpose(d_ps[:, t, :], d_cols[:, at : at + PAIR * P - 1 : PAIR], ident[:])
             nc.scalar.copy(out=d_words[:, g * PACK : (g + 1) * PACK], in_=d_ps[:, :, 0])
 
-        def scale_blocks(k, b):
-            if b == 0:
-                a_hat = hat_pool.tile([P, 2, CHUNK], BF16)
+        def scale_half(k, half):
+            r, n, g, m = order[k]
+            if half == 0:
+                a_hat = hat_pool.tile([P, UNIT_PASSES * K_PASS], BF16)
                 hat_tiles[k] = a_hat
-            elif one_row_tile(k):
-                return
-            n = 2 if one_row_tile(k) else 1
-            r, c = order[k][b]
-            nc.vector.scalar_tensor_tensor(
-                out=hat_tiles[k][:, b : b + n, :].rearrange("p b j -> p (b j)"),
-                in0=x_tiles[k][:, b : b + n, :].rearrange("p b j -> p (b j)"),
-                scalar=d_rows[:, r : r + 1],
-                in1=d_cols[:, c * CHUNK : (c + n) * CHUNK],
-                op0=ALU.mult,
-                op1=ALU.mult,
-            )
+            for b in range((n * half + 1) // 2, (n * (half + 1) + 1) // 2):
+                nc.vector.scalar_tensor_tensor(
+                    out=hat_tiles[k][:, b * m * K_PASS : (b + 1) * m * K_PASS],
+                    in0=x_tiles[k][:, b, :],
+                    scalar=d_rows[:, r + b : r + b + 1],
+                    in1=d_cols[:, g * K_PASS : (g + m) * K_PASS],
+                    op0=ALU.mult,
+                    op1=ALU.mult,
+                )
 
-        def transpose_block(k, b):
-            words = hat_tiles[k][:, b, :].bitcast(F32)
-            a_ps = psum_t.tile([P, CHUNK_PASSES, PAIR, P], F32, tag="tp")
-            for g in range(CHUNK_PASSES):
+        def transpose_half(k, half):
+            words = hat_tiles[k][:].bitcast(F32)
+            a_ps = psum_t.tile([P, UNIT_PASSES // 2, PAIR, P], F32, tag="tp")
+            for s in range(UNIT_PASSES // 2):
                 for u in range(PAIR):
-                    at = (g * PAIR + u) * P
-                    nc.tensor.transpose(a_ps[:, g, u, :], words[:, at : at + P], ident[:])
-            transposed[(k, b)] = a_ps
+                    at = ((half * UNIT_PASSES // 2 + s) * PAIR + u) * P
+                    nc.tensor.transpose(a_ps[:, s, u, :], words[:, at : at + P], ident[:])
+            transposed[(k, half)] = a_ps
 
-        def group_words(k, b):
-            if b == 0:
-                grouped = grouped_pool.tile([P, 2 * CHUNK_PASSES, P, PACK], BF16, align_bytes=64)
+        def group_words(k, half):
+            if half == 0:
+                grouped = grouped_pool.tile([P, UNIT_PASSES, P, PACK], BF16, align_bytes=64)
                 grouped_tiles[k] = grouped
-            words = grouped_tiles[k][:].rearrange("p g i t -> p (g i t)").bitcast(F32)
-            n = CHUNK // PAIR
+            words = grouped_tiles[k][:].rearrange("p s i t -> p (s i t)").bitcast(F32)
+            n = UNIT_PASSES // 2 * PAIR * P
             nc.scalar.copy(
-                out=words[:, b * n : (b + 1) * n].rearrange("p (g i u) -> p g i u", i=P, u=PAIR),
-                in_=transposed[(k, b)][:].rearrange("p g u i -> p g i u"),
+                out=words[:, half * n : (half + 1) * n].rearrange("p (s i u) -> p s i u", i=P, u=PAIR),
+                in_=transposed[(k, half)][:].rearrange("p s u i -> p s i u"),
             )
 
         def quantise(k):
-            a_codes = codes_pool.tile([P, 2 * CHUNK_PASSES, P], U32, align_bytes=64)
-            a_scales = codes_pool.tile([P, 2 * CHUNK_PASSES, P], U8, align_bytes=64)
+            r, n, g, m = order[k]
+            a_codes = codes_pool.tile([P, UNIT_PASSES, P], U32, align_bytes=64)
+            a_scales = codes_pool.tile([P, UNIT_PASSES, P], U8, align_bytes=64)
             nc.vector.quantize_mx(
-                out=a_codes[:].rearrange("p g i -> p (g i)").bitcast(FP8X4),
-                scales=a_scales[:].rearrange("p g i -> p (g i)"),
-                in_=grouped_tiles[k][:].rearrange("p g i t -> p (g i t)"),
+                out=a_codes[:].rearrange("p s i -> p (s i)").bitcast(FP8X4),
+                scales=a_scales[:].rearrange("p s i -> p (s i)"),
+                in_=grouped_tiles[k][:].rearrange("p s i t -> p (s i t)"),
             )
-            for b, (r, c) in enumerate(order[k]):
-                for g in range(CHUNK_PASSES):
-                    at = b * CHUNK_PASSES + g
-                    code_tiles[(r, c * CHUNK_PASSES + g)] = (a_codes[:, at, :], a_scales[:, at, :])
+            for b in range(n):
+                for h in range(m):
+                    s = b * m + h
+                    code_tiles[(r + b, g + h)] = (a_codes[:, s, :], a_scales[:, s, :])
 
         def multiply_row_tile(r):
             bank, slot = divmod(r, TILES_PER_BANK)
-            if slot == 0:
+            if bank not in sum_tiles:
                 y_ps = psum_acc.tile([P, TILES_PER_BANK, N_OUT], F32, tag="acc")
-                sum_tiles.append(y_ps)
+                sum_tiles[bank] = y_ps
             for z_pass in range(PASSES):
                 codes, scales = code_tiles[(r, z_pass)]
                 nc.tensor.matmul_mx(
@@ -327,7 +351,7 @@ def tile_gcnlayer_pb_t_kernel(tc, A1, Hn, Wout, bout, out):
         def copy_sums(bank):
             y_sb = ypool.tile([P, TILES_PER_BANK * N_OUT], F32)
             nc.scalar.copy(out=y_sb[:], in_=sum_tiles[bank][:].rearrange("p r o -> p (r o)"))
-            copy_tiles.append(y_sb)
+            copy_tiles[bank] = y_sb
 
         def leaky_relu_and_store(bank):
             result = ypool.tile([P, TILES_PER_BANK, N_OUT], F32)
@@ -344,42 +368,51 @@ def tile_gcnlayer_pb_t_kernel(tc, A1, Hn, Wout, bout, out):
                 out=out_tiles[:, first_tile : first_tile + TILES_PER_BANK, :], in_=result[:]
             )
 
-        def ends_row_tile(k, every):
-            if 0 <= k < len(order):
-                r, c = order[k][1]
-                if c == GROUPS - 1 and r % every == every - 1:
-                    return r
-            return None
+        passes_left = {r: PASSES for r in range(ROW_TILES)}
+        tiles_left = {bank: TILES_PER_BANK for bank in range(ROW_TILES // TILES_PER_BANK)}
+        completed_tiles = []
+        completed_banks = []
+        for r, n, g, m in order:
+            tiles = []
+            banks = []
+            for tile in range(r, r + n):
+                passes_left[tile] -= m
+                if passes_left[tile] == 0:
+                    tiles.append(tile)
+                    tiles_left[tile // TILES_PER_BANK] -= 1
+                    if tiles_left[tile // TILES_PER_BANK] == 0:
+                        banks.append(tile // TILES_PER_BANK)
+            completed_tiles.append(tiles)
+            completed_banks.append(banks)
+
+        def behind(completed, k):
+            return completed[k] if 0 <= k < len(order) else []
 
         def work_on_unit(k):
             if k + X_AHEAD < len(order):
                 fetch_unit(k + X_AHEAD)
             if by_scalar(k + 2):
                 scale_rows(k + 2)
-            for b in range(2):
+            for half in range(2):
                 if k < len(order) and not by_scalar(k):
-                    scale_blocks(k, b)
-                    transpose_block(k, b)
-                done = k - 1 + b
+                    scale_half(k, half)
+                    transpose_half(k, half)
+                done = k - 1 + half
                 if 0 <= done < len(order) and not by_scalar(done):
-                    group_words(done, 1 - b)
+                    group_words(done, 1 - half)
                 if by_scalar(k + 1):
-                    scale_columns(k + 1, b)
-                if b == 0:
+                    scale_columns(k + 1, half)
+                if half == 0:
                     if by_scalar(k):
                         interleave(k)
                     if 0 <= k - QUANT_LAG < len(order):
                         quantise(k - QUANT_LAG)
-            r = ends_row_tile(k - MATMUL_LAG, TILES_PER_RUN)
-            if r is not None:
-                for tile in range(r - TILES_PER_RUN + 1, r + 1):
-                    multiply_row_tile(tile)
-            r = ends_row_tile(k - YCOPY_LAG, TILES_PER_BANK)
-            if r is not None:
-                copy_sums(r // TILES_PER_BANK)
-            r = ends_row_tile(k - STORE_LAG, TILES_PER_BANK)
-            if r is not None:
-                leaky_relu_and_store(r // TILES_PER_BANK)
+            for tile in behind(completed_tiles, k - MATMUL_LAG):
+                multiply_row_tile(tile)
+            for bank in behind(completed_banks, k - YCOPY_LAG):
+                copy_sums(bank)
+            for bank in behind(completed_banks, k - STORE_LAG):
+                leaky_relu_and_store(bank)
 
         hn_tiles = []
         h_grouped_tiles = []
@@ -520,7 +553,7 @@ def tile_gcnlayer_pb_t_kernel(tc, A1, Hn, Wout, bout, out):
             w_codes = zkeep.tile([P, N_OUT], U32, align_bytes=64)
             w_scales = zkeep.tile([P, N_OUT], U8, align_bytes=64)
             k = run_steps(-ROW_AHEAD, Z_LAST, 0)
-        offload_pool = ctx.enter_context(tc.tile_pool(name="offload_pool", bufs=2))
+        offload_pool = ctx.enter_context(tc.tile_pool(name="offload_pool", bufs=1))
         ypool = ctx.enter_context(tc.tile_pool(name="ypool", bufs=2))
         k = run_steps(Z_LAST, ROW_TILES + D_LAG, k)
         while k < len(order) + STORE_LAG:

@@ -44,7 +44,7 @@ D_LAG = 2
 Z_FIRST = 0
 Z_LAST = Z_FIRST + PASSES + 3
 UNIT_PASSES = 4
-CODES_BUFS = 41
+CODES_BUFS = 40
 OFFLOAD_EVERY = 2
 
 
@@ -85,7 +85,9 @@ def tile_gcnlayer_pb_t_kernel(tc, A1, Hn, Wout, bout, out):
         grouped_pool = ctx.enter_context(tc.tile_pool(name="grouped_pool", bufs=QUANT_LAG + 2))
         dpool = ctx.enter_context(tc.tile_pool(name="dpool", bufs=2))
         codes_pool = ctx.enter_context(tc.tile_pool(name="codes_pool", bufs=CODES_BUFS))
-        psum_t = ctx.enter_context(tc.psum_pool(name="psum_t", bufs=6))
+        psum_t = ctx.enter_context(tc.psum_pool(name="psum_t", bufs=5))
+        psum_busy = ctx.enter_context(tc.psum_pool(name="psum_busy", bufs=1))
+        busy = psum_busy.tile([P, P], F32)
         psum_acc = ctx.enter_context(tc.psum_pool(name="psum_acc", bufs=2))
 
         ident = keep.tile([P, P], F32)
@@ -174,7 +176,8 @@ def tile_gcnlayer_pb_t_kernel(tc, A1, Hn, Wout, bout, out):
         def d_of_chunk(q):
             d_along_columns(q)
             for g in range(FIRST_TILE[q] // PACK, FIRST_TILE[q + 1] // PACK):
-                d_along_words(g)
+                if g in word_passes:
+                    d_along_words(g)
 
         def rectangles(r, r_end, g, g_end):
             units = []
@@ -194,7 +197,11 @@ def tile_gcnlayer_pb_t_kernel(tc, A1, Hn, Wout, bout, out):
         by_group[-1] = mixed(by_group[-1])
         by_group[-2] = mixed(by_group[-2])
         order = [unit for fresh in by_group for unit in fresh]
+        first_late = len(order) - len(by_group[-1])
         scalar_units = scalar_units_of(order, by_group)
+        word_passes = set()
+        for k in scalar_units:
+            word_passes = word_passes | set(range(order[k][2], order[k][2] + order[k][3]))
 
         def units_at_step(step):
             for q in range(GROUPS - 1):
@@ -302,6 +309,8 @@ def tile_gcnlayer_pb_t_kernel(tc, A1, Hn, Wout, bout, out):
                 for u in range(PAIR):
                     at = ((half * UNIT_PASSES // 2 + s) * PAIR + u) * P
                     nc.tensor.transpose(a_ps[:, s, u, :], words[:, at : at + P], ident[:])
+            if k >= first_late:
+                nc.tensor.matmul(busy[:], lhsT=words[:, at : at + P], rhs=ident[:], start=True, stop=True)
             transposed[(k, half)] = a_ps
 
         def group_words(k, half):
@@ -426,6 +435,14 @@ def tile_gcnlayer_pb_t_kernel(tc, A1, Hn, Wout, bout, out):
                     in_=Wout[256 * u : 256 * (u + 1), :].rearrange("(p e) o -> p e o", e=PAIR),
                 )
 
+        def load_bias():
+            nc.vector.memset(bias_rows[:], 0.0)
+            nc.sync.dma_start(out=bias_rows[0:1, :], in_=bout.unsqueeze(0))
+            nc.vector.memset(ones[:], 1.0)
+            bias_ps = psum_t.tile([P, N_OUT], F32, tag="tp")
+            nc.tensor.matmul(bias_ps[:], lhsT=ones[:], rhs=bias_rows[:], start=True, stop=True)
+            nc.scalar.copy(out=bias_bc[:], in_=bias_ps[:])
+
         def load_h(g):
             hn = hpool.tile([P, PACK, N_FEAT], BF16)
             nc.sync.dma_start(
@@ -514,7 +531,7 @@ def tile_gcnlayer_pb_t_kernel(tc, A1, Hn, Wout, bout, out):
                 if z + Z_AHEAD == 0:
                     load_w()
                 if z + Z_AHEAD == 1:
-                    nc.sync.dma_start(out=bias_bc[:], in_=bout.partition_broadcast(P))
+                    load_bias()
                 if 0 <= z + Z_AHEAD < PASSES:
                     load_h(z + Z_AHEAD)
                 if step == FETCH_STEP:
@@ -548,7 +565,9 @@ def tile_gcnlayer_pb_t_kernel(tc, A1, Hn, Wout, bout, out):
 
         with tc.tile_pool(name="zkeep", bufs=1) as zkeep, tc.tile_pool(name="zstage", bufs=2) as zstage, tc.tile_pool(name="hpool", bufs=Z_AHEAD + 1) as hpool:
             w_raw = zkeep.tile([P, PACK, N_OUT], BF16)
-            bias_bc = zkeep.tile([P, N_OUT], BF16)
+            bias_bc = zkeep.tile([P, N_OUT], F32)
+            bias_rows = zkeep.tile([P, N_OUT], BF16)
+            ones = zkeep.tile([P, P], BF16)
             w_grouped = zkeep.tile([P, N_OUT, PACK], BF16, align_bytes=64)
             w_codes = zkeep.tile([P, N_OUT], U32, align_bytes=64)
             w_scales = zkeep.tile([P, N_OUT], U8, align_bytes=64)

from contextlib import ExitStack

import concourse.mybir as mybir
from concourse.masks import make_identity

F32 = mybir.dt.float32
BF16 = mybir.dt.bfloat16
U32 = mybir.dt.uint32
U8 = mybir.dt.uint8
FP8X4 = mybir.dt.float8_e4m3fn_x4
ALU = mybir.AluOpType
ACT = mybir.ActivationFunctionType

P = 128
PACK = 4
PAIR = 2
K_PASS = P * PACK
N_NODES = 4096
N_FEAT = 512
N_OUT = 128
LEAKY_SLOPE = 0.01

ROW_TILES = N_NODES // P
PASSES = N_NODES // K_PASS
GROUP_TILES = (4, 4, 8, 8, 8)
VECTOR_SUM_COLS = (3072, 3072, 2304, 1536, 256)
GROUPS = len(GROUP_TILES)
FIRST_TILE = [sum(GROUP_TILES[:q]) for q in range(GROUPS + 1)]
GROUP_OF = [q for q in range(GROUPS) for r in range(GROUP_TILES[q])]
TILES_PER_BANK = 4

ROW_AHEAD = 4
Z_AHEAD = 2
X_AHEAD = 3
COPY_LAG = 1
QUANT_LAG = 2
MATMUL_LAG = 3
YCOPY_LAG = 4
STORE_LAG = 6
OFFLOAD_LEAD = 2
FETCH_STEP = 3
EARLY_OFFLOADS = 0
D_LAG = 2
Z_FIRST = 0
Z_LAST = Z_FIRST + PASSES + 3
UNIT_PASSES = 4
CODES_BUFS = 40
OFFLOAD_EVERY = 2


def mixed(units):
    several = [unit for unit in units if unit[1] > 1]
    single = [unit for unit in units if unit[1] == 1]
    result = []
    taken = 0
    for i in range(len(units)):
        if taken < len(several) and taken * len(units) <= i * len(several):
            result.append(several[taken])
            taken += 1
        else:
            result.append(single[i - taken])
    return result


def scalar_units_of(order, by_group):
    first_late = len(order) - len(by_group[-1])
    several = [k for k in range(first_late, len(order)) if order[k][1] > 1]
    units = several[OFFLOAD_EVERY - 1 :: OFFLOAD_EVERY]
    first = first_late - len(by_group[-2])
    several = [k for k in range(first, first_late) if order[k][1] > 1]
    units.extend(several[len(several) - EARLY_OFFLOADS :])
    return set(units)


FLOPS = 2 * N_NODES * N_FEAT * N_OUT + 2 * N_NODES * N_NODES * N_OUT


def tile_gcnlayer_pb_t_kernel(tc, A1, Hn, Wout, bout, out):
    nc = tc.nc
    with ExitStack() as ctx:
        keep = ctx.enter_context(tc.tile_pool(name="keep", bufs=1))
        rowpool = ctx.enter_context(tc.tile_pool(name="rowpool", bufs=ROW_AHEAD + 1))
        xpool = ctx.enter_context(tc.tile_pool(name="xpool", bufs=X_AHEAD + 2))
        hat_pool = ctx.enter_context(tc.tile_pool(name="hat_pool", bufs=2))
        grouped_pool = ctx.enter_context(tc.tile_pool(name="grouped_pool", bufs=QUANT_LAG + 2))
        dpool = ctx.enter_context(tc.tile_pool(name="dpool", bufs=2))
        codes_pool = ctx.enter_context(tc.tile_pool(name="codes_pool", bufs=CODES_BUFS))
        psum_t = ctx.enter_context(tc.psum_pool(name="psum_t", bufs=5))
        psum_busy = ctx.enter_context(tc.psum_pool(name="psum_busy", bufs=1))
        busy = psum_busy.tile([P, P], F32)
        psum_acc = ctx.enter_context(tc.psum_pool(name="psum_acc", bufs=2))

        ident = keep.tile([P, P], F32)
        make_identity(nc, ident[:])

        one = keep.tile([P, 1], F32)
        nc.vector.memset(one[:], 1.0)
        warm = keep.tile([P, 1], F32)
        nc.scalar.activation(out=warm[:], in_=one[:], func=ACT.Abs_reciprocal_sqrt)

        z_codes = keep.tile([P, PASSES, N_OUT], U32, align_bytes=64)
        z_scales = keep.tile([P, PASSES, N_OUT], U8, align_bytes=64)
        d_rows = keep.tile([P, ROW_TILES], F32)
        d_words = keep.tile([P, ROW_TILES], F32)
        d_cols = keep.tile([P, N_NODES], F32)
        sums_v = keep.tile([P, ROW_TILES], F32)
        sums_s = keep.tile([P, ROW_TILES], F32)

        row_tiles = []

        def load_rows(r):
            rows = rowpool.tile([P, N_NODES], BF16)
            nc.sync.dma_start(out=rows[:], in_=A1[r * P : (r + 1) * P, :])
            row_tiles.append(rows)

        def sum_rows_vector(r):
            part = row_tiles[r][:, : VECTOR_SUM_COLS[GROUP_OF[r]]]
            nc.vector.tensor_scalar(
                out=part,
                in0=part,
                scalar1=1.0,
                scalar2=None,
                op0=ALU.mult,
                op1=ALU.add,
                accum_out=sums_v[:, r : r + 1],
            )

        def sum_rows_scalar(r):
            part = row_tiles[r][:, VECTOR_SUM_COLS[GROUP_OF[r]] :]
            nc.scalar.activation(out=part, in_=part, func=ACT.Copy, accum_out=sums_s[:, r : r + 1])

        d_parts = {}

        def add_row_sums(q):
            tiles = slice(FIRST_TILE[q], FIRST_TILE[q + 1])
            rowsum = dpool.tile([P, GROUP_TILES[q]], F32)
            nc.vector.tensor_tensor(out=rowsum[:], in0=sums_v[:, tiles], in1=sums_s[:, tiles], op=ALU.add)
            guess = dpool.tile([P, GROUP_TILES[q]], F32)
            nc.scalar.activation(out=guess[:], in_=rowsum[:], func=ACT.Abs_reciprocal_sqrt)
            d_parts[q] = (rowsum, guess)

        def square_guess(q):
            rowsum, guess = d_parts[q]
            square = dpool.tile([P, GROUP_TILES[q]], F32)
            nc.vector.tensor_tensor(out=square[:], in0=guess[:], in1=guess[:], op=ALU.mult)
            d_parts[q] = (rowsum, guess, square)

        def half_product(q):
            rowsum, guess, square = d_parts[q]
            product = dpool.tile([P, GROUP_TILES[q]], F32)
            nc.vector.scalar_tensor_tensor(
                out=product[:], in0=square[:], scalar=-0.5, in1=rowsum[:], op0=ALU.mult, op1=ALU.mult
            )
            d_parts[q] = (guess, product)

        def d_of_rows(q):
            guess, product = d_parts[q]
            tiles = slice(FIRST_TILE[q], FIRST_TILE[q + 1])
            nc.vector.scalar_tensor_tensor(
                out=d_rows[:, tiles], in0=product[:], scalar=1.5, in1=guess[:], op0=ALU.add, op1=ALU.mult
            )

        def d_along_columns(q):
            for first in range(FIRST_TILE[q], FIRST_TILE[q + 1], TILES_PER_BANK):
                d_ps = psum_t.tile([P, TILES_PER_BANK, P], F32, tag="tp")
                for a in range(TILES_PER_BANK):
                    r = first + a
                    nc.tensor.transpose(
                        d_ps[:, a, :], d_rows[:, r : r + 1].to_broadcast([P, P]), ident[:]
                    )
                nc.scalar.copy(
                    out=d_cols[:, first * P : (first + TILES_PER_BANK) * P],
                    in_=d_ps[:].rearrange("p a n -> p (a n)"),
                )

        def d_of_chunk(q):
            d_along_columns(q)
            for g in range(FIRST_TILE[q] // PACK, FIRST_TILE[q + 1] // PACK):
                if g in word_passes:
                    d_along_words(g)

        def rectangles(r, r_end, g, g_end):
            units = []
            for m in (4, 2, 1):
                n = UNIT_PASSES // m
                while g_end - g >= m:
                    units.extend([(first, n, g, m) for first in range(r, r_end, n)])
                    g += m
            return units

        by_group = []
        for q in range(GROUPS):
            first, last = FIRST_TILE[q], FIRST_TILE[q + 1]
            fresh = rectangles(0, first, first // PACK, last // PACK)
            fresh.extend(rectangles(first, last, 0, last // PACK))
            by_group.append(fresh)
        by_group[-1] = mixed(by_group[-1])
        by_group[-2] = mixed(by_group[-2])
        order = [unit for fresh in by_group for unit in fresh]
        first_late = len(order) - len(by_group[-1])
        scalar_units = scalar_units_of(order, by_group)
        word_passes = set()
        for k in scalar_units:
            word_passes = word_passes | set(range(order[k][2], order[k][2] + order[k][3]))

        def units_at_step(step):
            for q in range(GROUPS - 1):
                s = step - FIRST_TILE[q + 1] - D_LAG
                n = GROUP_TILES[q + 1]
                if 0 <= s < n:
                    return len(by_group[q]) * (s + 1) // n - len(by_group[q]) * s // n
            return 0

        x_tiles = []
        grouped_tiles = {}
        hat_tiles = {}
        transposed = {}
        code_tiles = {}
        sum_tiles = {}
        copy_tiles = {}

        def fetch_unit(k):
            r, n, g, m = order[k]
            x = xpool.tile([P, n, m * K_PASS], BF16)
            nc.sync.dma_start(
                out=x[:],
                in_=A1[r * P : (r + n) * P, g * K_PASS : (g + m) * K_PASS].rearrange(
                    "(b p) j -> p b j", p=P
                ),
            )
            x_tiles.append(x)

        def by_scalar(k):
            return k in scalar_units

        scaled_rows = {}
        scaled_columns = {}

        def scale_rows(k):
            r, n, g, m = order[k]
            half_hat = offload_pool.tile([P, n, m * PAIR, PAIR, P], F32)
            for b in range(n):
                nc.scalar.activation(
                    out=half_hat[:, b, :, :, :],
                    in_=x_tiles[k][:, b, :].rearrange("i (w p e) -> i w e p", p=P, e=PAIR),
                    func=ACT.Copy,
                    scale=d_rows[:, r + b : r + b + 1],
                )
            scaled_rows[k] = half_hat
            hat_columns = offload_pool.tile([P, n, m, PACK, P], BF16)
            scaled_columns[k] = hat_columns

        def scale_columns(k, half):
            r, n, g, m = order[k]
            values = [(h, t) for h in range(m) for t in range(PACK)]
            values = values[len(values) * half // 2 : len(values) * (half + 1) // 2]
            in_bank = TILES_PER_BANK // n
            for first in range(0, len(values), in_bank):
                t_ps = psum_t.tile([P, in_bank, n, P], F32, tag="tp")
                for s in range(in_bank):
                    h, t = values[first + s]
                    u, e = divmod(t, PAIR)
                    for b in range(n):
                        nc.tensor.transpose(t_ps[:, s, b, :], scaled_rows[k][:, b, h * PAIR + u, e, :], ident[:])
                for s in range(in_bank):
                    h, t = values[first + s]
                    at = (g + h) * PACK + t
                    nc.scalar.activation(
                        out=scaled_columns[k][:, :, h, t, :],
                        in_=t_ps[:, s, :, :],
                        func=ACT.Copy,
                        scale=d_words[:, at : at + 1],
                    )

        def interleave(k):
            grouped = grouped_pool.tile([P, UNIT_PASSES, P, PACK], BF16, align_bytes=64)
            nc.scalar.copy(
                out=grouped[:], in_=scaled_columns[k][:].rearrange("p b h t i -> p (b h) i t")
            )
            grouped_tiles[k] = grouped

        def d_along_words(g):
            d_ps = psum_t.tile([P, PACK, P], F32, tag="tp")
            for t in range(PACK):
                u, e = divmod(t, PAIR)
                at = (g * PAIR + u) * PAIR * P + e
                nc.tensor.transpose(d_ps[:, t, :], d_cols[:, at : at + PAIR * P - 1 : PAIR], ident[:])
            nc.scalar.copy(out=d_words[:, g * PACK : (g + 1) * PACK], in_=d_ps[:, :, 0])

        def scale_half(k, half):
            r, n, g, m = order[k]
            if half == 0:
                a_hat = hat_pool.tile([P, UNIT_PASSES * K_PASS], BF16)
                hat_tiles[k] = a_hat
            for b in range((n * half + 1) // 2, (n * (half + 1) + 1) // 2):
                nc.vector.scalar_tensor_tensor(
                    out=hat_tiles[k][:, b * m * K_PASS : (b + 1) * m * K_PASS],
                    in0=x_tiles[k][:, b, :],
                    scalar=d_rows[:, r + b : r + b + 1],
                    in1=d_cols[:, g * K_PASS : (g + m) * K_PASS],
                    op0=ALU.mult,
                    op1=ALU.mult,
                )

        def transpose_half(k, half):
            words = hat_tiles[k][:].bitcast(F32)
            a_ps = psum_t.tile([P, UNIT_PASSES // 2, PAIR, P], F32, tag="tp")
            for s in range(UNIT_PASSES // 2):
                for u in range(PAIR):
                    at = ((half * UNIT_PASSES // 2 + s) * PAIR + u) * P
                    nc.tensor.transpose(a_ps[:, s, u, :], words[:, at : at + P], ident[:])
            if k >= first_late:
                nc.tensor.matmul(busy[:], lhsT=words[:, at : at + P], rhs=ident[:], start=True, stop=True)
            transposed[(k, half)] = a_ps

        def group_words(k, half):
            if half == 0:
                grouped = grouped_pool.tile([P, UNIT_PASSES, P, PACK], BF16, align_bytes=64)
                grouped_tiles[k] = grouped
            words = grouped_tiles[k][:].rearrange("p s i t -> p (s i t)").bitcast(F32)
            n = UNIT_PASSES // 2 * PAIR * P
            nc.scalar.copy(
                out=words[:, half * n : (half + 1) * n].rearrange("p (s i u) -> p s i u", i=P, u=PAIR),
                in_=transposed[(k, half)][:].rearrange("p s u i -> p s i u"),
            )

        def quantise(k):
            r, n, g, m = order[k]
            a_codes = codes_pool.tile([P, UNIT_PASSES, P], U32, align_bytes=64)
            a_scales = codes_pool.tile([P, UNIT_PASSES, P], U8, align_bytes=64)
            nc.vector.quantize_mx(
                out=a_codes[:].rearrange("p s i -> p (s i)").bitcast(FP8X4),
                scales=a_scales[:].rearrange("p s i -> p (s i)"),
                in_=grouped_tiles[k][:].rearrange("p s i t -> p (s i t)"),
            )
            for b in range(n):
                for h in range(m):
                    s = b * m + h
                    code_tiles[(r + b, g + h)] = (a_codes[:, s, :], a_scales[:, s, :])

        def multiply_row_tile(r):
            bank, slot = divmod(r, TILES_PER_BANK)
            if bank not in sum_tiles:
                y_ps = psum_acc.tile([P, TILES_PER_BANK, N_OUT], F32, tag="acc")
                sum_tiles[bank] = y_ps
            for z_pass in range(PASSES):
                codes, scales = code_tiles[(r, z_pass)]
                nc.tensor.matmul_mx(
                    out=sum_tiles[bank][:, slot, :],
                    lhsT=codes.bitcast(FP8X4),
                    lhsT_scale=scales,
                    rhs=z_codes[:, z_pass, :].bitcast(FP8X4),
                    rhs_scale=z_scales[:, z_pass, :],
                    start=(z_pass == 0),
                    stop=(z_pass == PASSES - 1),
                )

        out_tiles = out.rearrange("(r p) o -> p r o", p=P)

        def copy_sums(bank):
            y_sb = ypool.tile([P, TILES_PER_BANK * N_OUT], F32)
            nc.scalar.copy(out=y_sb[:], in_=sum_tiles[bank][:].rearrange("p r o -> p (r o)"))
            copy_tiles[bank] = y_sb

        def leaky_relu_and_store(bank):
            result = ypool.tile([P, TILES_PER_BANK, N_OUT], F32)
            nc.vector.scalar_tensor_tensor(
                out=result[:].rearrange("p r o -> p (r o)"),
                in0=sum_tiles[bank][:].rearrange("p r o -> p (r o)"),
                scalar=LEAKY_SLOPE,
                in1=copy_tiles[bank][:],
                op0=ALU.mult,
                op1=ALU.max,
            )
            first_tile = bank * TILES_PER_BANK
            nc.sync.dma_start(
                out=out_tiles[:, first_tile : first_tile + TILES_PER_BANK, :], in_=result[:]
            )

        passes_left = {r: PASSES for r in range(ROW_TILES)}
        tiles_left = {bank: TILES_PER_BANK for bank in range(ROW_TILES // TILES_PER_BANK)}
        completed_tiles = []
        completed_banks = []
        for r, n, g, m in order:
            tiles = []
            banks = []
            for tile in range(r, r + n):
                passes_left[tile] -= m
                if passes_left[tile] == 0:
                    tiles.append(tile)
                    tiles_left[tile // TILES_PER_BANK] -= 1
                    if tiles_left[tile // TILES_PER_BANK] == 0:
                        banks.append(tile // TILES_PER_BANK)
            completed_tiles.append(tiles)
            completed_banks.append(banks)

        def behind(completed, k):
            return completed[k] if 0 <= k < len(order) else []

        def work_on_unit(k):
            if k + X_AHEAD < len(order):
                fetch_unit(k + X_AHEAD)
            if by_scalar(k + 2):
                scale_rows(k + 2)
            for half in range(2):
                if k < len(order) and not by_scalar(k):
                    scale_half(k, half)
                    transpose_half(k, half)
                done = k - 1 + half
                if 0 <= done < len(order) and not by_scalar(done):
                    group_words(done, 1 - half)
                if by_scalar(k + 1):
                    scale_columns(k + 1, half)
                if half == 0:
                    if by_scalar(k):
                        interleave(k)
                    if 0 <= k - QUANT_LAG < len(order):
                        quantise(k - QUANT_LAG)
            for tile in behind(completed_tiles, k - MATMUL_LAG):
                multiply_row_tile(tile)
            for bank in behind(completed_banks, k - YCOPY_LAG):
                copy_sums(bank)
            for bank in behind(completed_banks, k - STORE_LAG):
                leaky_relu_and_store(bank)

        hn_tiles = []
        h_grouped_tiles = []
        z_sums = []
        z_tiles = []

        def load_w():
            for u in range(PAIR):
                nc.sync.dma_start(
                    out=w_raw[:, PAIR * u : PAIR * (u + 1), :],
                    in_=Wout[256 * u : 256 * (u + 1), :].rearrange("(p e) o -> p e o", e=PAIR),
                )

        def load_bias():
            nc.vector.memset(bias_rows[:], 0.0)
            nc.sync.dma_start(out=bias_rows[0:1, :], in_=bout.unsqueeze(0))
            nc.vector.memset(ones[:], 1.0)
            bias_ps = psum_t.tile([P, N_OUT], F32, tag="tp")
            nc.tensor.matmul(bias_ps[:], lhsT=ones[:], rhs=bias_rows[:], start=True, stop=True)
            nc.scalar.copy(out=bias_bc[:], in_=bias_ps[:])

        def load_h(g):
            hn = hpool.tile([P, PACK, N_FEAT], BF16)
            nc.sync.dma_start(
                out=hn[:].rearrange("m (u e) f -> m u e f", e=PAIR),
                in_=Hn[g * K_PASS : (g + 1) * K_PASS, :].rearrange("(u m e) f -> m u e f", m=P, e=PAIR),
            )
            hn_tiles.append(hn)

        def transpose_h(g):
            words = hn_tiles[g][:].rearrange("m t f -> m (t f)").bitcast(F32)
            h_grouped = zstage.tile([P, PACK * P * PACK], BF16, align_bytes=64)
            h_words = h_grouped[:].bitcast(F32).rearrange("p (t m u) -> p t m u", m=P, u=PAIR)
            for half in range(2):
                h_ps = psum_t.tile([P, PAIR, PAIR, P], F32, tag="tp")
                for a in range(PAIR):
                    for u in range(PAIR):
                        first = ((half * PAIR + a) * PAIR + u) * P
                        nc.tensor.transpose(h_ps[:, a, u, :], words[:, first : first + P], ident[:])
                nc.scalar.copy(
                    out=h_words[:, half * PAIR : (half + 1) * PAIR, :, :],
                    in_=h_ps[:].rearrange("p a u m -> p a m u"),
                )
            h_grouped_tiles.append(h_grouped)

        def multiply_h(g):
            h_codes = zstage.tile([P, PACK, P], U32, align_bytes=64)
            h_scales = zstage.tile([P, PACK, P], U8, align_bytes=64)
            nc.vector.quantize_mx(
                out=h_codes[:].rearrange("p t m -> p (t m)").bitcast(FP8X4),
                scales=h_scales[:].rearrange("p t m -> p (t m)"),
                in_=h_grouped_tiles[g][:],
            )
            z_ps = psum_acc.tile([P, PACK, N_OUT], F32, tag="acc")
            for t in range(PACK):
                nc.tensor.matmul_mx(
                    out=z_ps[:, t, :],
                    lhsT=h_codes[:, t, :].bitcast(FP8X4),
                    lhsT_scale=h_scales[:, t, :],
                    rhs=w_codes[:].bitcast(FP8X4),
                    rhs_scale=w_scales[:],
                    start=True,
                    stop=True,
                )
            z_sums.append(z_ps)

        def add_bias(g):
            z_grouped = zstage.tile([P, N_OUT, PACK], BF16, align_bytes=64)
            nc.vector.tensor_tensor(
                out=z_grouped[:],
                in0=z_sums[g][:].rearrange("p t o -> p o t"),
                in1=bias_bc[:].unsqueeze(2).to_broadcast([P, N_OUT, PACK]),
                op=ALU.add,
            )
            z_tiles.append(z_grouped)

        def quantise_z(g):
            nc.vector.quantize_mx(
                out=z_codes[:, g, :].bitcast(FP8X4),
                scales=z_scales[:, g, :],
                in_=z_tiles[g][:].rearrange("p o t -> p (o t)"),
            )

        def work_on_z(z):
            if z == 0:
                nc.vector.tensor_copy(out=w_grouped[:], in_=w_raw[:].rearrange("p t o -> p o t"))
            if 0 <= z < PASSES:
                transpose_h(z)
            if z == 1:
                nc.vector.quantize_mx(
                    out=w_codes[:].bitcast(FP8X4),
                    scales=w_scales[:],
                    in_=w_grouped[:].rearrange("p o t -> p (o t)"),
                )
            if 0 <= z - 1 < PASSES:
                multiply_h(z - 1)
            if 0 <= z - 2 < PASSES:
                add_bias(z - 2)
            if 0 <= z - 3 < PASSES:
                quantise_z(z - 3)

        def run_steps(first_step, last_step, k):
            for step in range(first_step, last_step):
                if step + ROW_AHEAD < ROW_TILES:
                    load_rows(step + ROW_AHEAD)
                z = step - Z_FIRST
                if z + Z_AHEAD == 0:
                    load_w()
                if z + Z_AHEAD == 1:
                    load_bias()
                if 0 <= z + Z_AHEAD < PASSES:
                    load_h(z + Z_AHEAD)
                if step == FETCH_STEP:
                    for ahead in range(X_AHEAD):
                        fetch_unit(ahead)
                if step < 0:
                    continue
                late = []
                for q in range(GROUPS):
                    s = step - FIRST_TILE[q + 1]
                    if s == 0:
                        late = [add_row_sums, square_guess, half_product, d_of_rows, d_of_chunk]
                    if late:
                        break
                if step < ROW_TILES:
                    sum_rows_vector(step)
                work_on_z(z)
                count = units_at_step(step)
                for i in range(count):
                    work_on_unit(k)
                    k += 1
                    if i == 0 and step < ROW_TILES:
                        sum_rows_scalar(step)
                    for small in late[i : i + 1]:
                        small(q)
                if count == 0 and step < ROW_TILES:
                    sum_rows_scalar(step)
                for small in late[count:]:
                    small(q)
            return k

        with tc.tile_pool(name="zkeep", bufs=1) as zkeep, tc.tile_pool(name="zstage", bufs=2) as zstage, tc.tile_pool(name="hpool", bufs=Z_AHEAD + 1) as hpool:
            w_raw = zkeep.tile([P, PACK, N_OUT], BF16)
            bias_bc = zkeep.tile([P, N_OUT], F32)
            bias_rows = zkeep.tile([P, N_OUT], BF16)
            ones = zkeep.tile([P, P], BF16)
            w_grouped = zkeep.tile([P, N_OUT, PACK], BF16, align_bytes=64)
            w_codes = zkeep.tile([P, N_OUT], U32, align_bytes=64)
            w_scales = zkeep.tile([P, N_OUT], U8, align_bytes=64)
            k = run_steps(-ROW_AHEAD, Z_LAST, 0)
        offload_pool = ctx.enter_context(tc.tile_pool(name="offload_pool", bufs=1))
        ypool = ctx.enter_context(tc.tile_pool(name="ypool", bufs=2))
        k = run_steps(Z_LAST, ROW_TILES + D_LAG, k)
        while k < len(order) + STORE_LAG:
            work_on_unit(k)
            k += 1
